import numpy as np
import ml_dtypes


def mxq(x, axis, fmt="e4m3"):
    dtype, down = {"e4m3": (ml_dtypes.float8_e4m3fn, 7), "e5m2": (ml_dtypes.float8_e5m2, 14)}[fmt]
    v = np.moveaxis(np.asarray(x, np.float32).astype(ml_dtypes.bfloat16).astype(np.float64), axis, -1)
    blocks = v.reshape(v.shape[:-1] + (-1, 32))
    amax = np.abs(blocks).max(-1, keepdims=True)
    byte = np.maximum(np.where(amax > 0, np.frexp(amax)[1] - 1 + 127, 0) - down, 1)
    scale = np.exp2(byte - 127.0)
    codes = (blocks / scale).astype(np.float32).astype(dtype).astype(np.float64)
    return np.moveaxis((codes * scale).reshape(v.shape), -1, axis)


WIDE = False


def mx_kscale(k):
    if not WIDE:
        return np.ones(k)
    levels = np.array([10, -10, 5, -5, 0])
    if k % 512:
        return np.exp2(np.random.permutation(np.resize(levels, k // 32))).repeat(32)
    a = np.empty((k // 512, 16))
    for p in range(k // 512):
        a[p, :8] = np.random.permutation(np.resize(levels, 8))
        for g in range(8):
            far = levels[np.abs(levels - a[p, g]) >= 10]
            a[p, g + 8] = far[np.random.randint(len(far))]
    return np.exp2(a.ravel()).repeat(32)


BF16 = ml_dtypes.bfloat16


def bf(x):
    return np.asarray(x, np.float32).astype(BF16)


def f64(x):
    return np.asarray(x).astype(np.float64)


B, N, R, I = 2, 2048, 128, 256
SIG = 1.5
P0 = 0.05
RM = np.exp(0.5 * SIG * SIG)


def draw_flows():
    keep = np.random.random((B, 1, N)) >= P0
    return keep * np.exp(SIG * np.random.standard_normal((B, N, N)) - 0.5 * SIG * SIG)


def setup_inputs():
    u = mx_kscale(N)
    return {"flows": bf(draw_flows() * u[None, :, None]),
            "x_gcn1": bf(np.random.standard_normal((B, N, R)) / u[None, :, None] * np.mean(u)),
            "W2": bf(np.random.standard_normal((R, I)) * 0.5 * np.sqrt(N) / (RM * np.sqrt(R))),
            "b2": bf(np.random.standard_normal(I) * 0.1)}


def reference(flows, x_gcn1, W2, b2):
    A = f64(flows)
    deg = A.sum(axis=1)
    dinv = np.where(deg > 0, 1.0 / np.sqrt(np.where(deg > 0, deg, 1.0)), 0.0)
    xw = f64(x_gcn1) @ f64(W2)
    msg = xw * dinv[..., None]
    out = mxq(A, 1, "e4m3").transpose(0, 2, 1) @ mxq(msg, 1, "e4m3")
    return out * dinv[..., None] + f64(b2)

@@ -1,0 +1,301 @@
+from contextlib import ExitStack
+
+import concourse.mybir as mybir
+from concourse.masks import make_identity
+
+F32 = mybir.dt.float32
+BF16 = mybir.dt.bfloat16
+U32 = mybir.dt.uint32
+U8 = mybir.dt.uint8
+FP8X4 = mybir.dt.float8_e4m3fn_x4
+ALU = mybir.AluOpType
+AXIS = mybir.AxisListType
+
+P = 128
+PACK = 4
+GRAPHS = 2
+NODES = 2048
+FEATURES = 128
+CHANNELS = 256
+PASSES = NODES // (P * PACK)
+NODE_TILES = NODES // P
+UNIT = 512
+UNITS = NODES // UNIT
+VECTOR_COLUMNS = (256, 64)
+RUN = 4
+HALF = CHANNELS // 2
+STORE_TILES = 2
+AHEAD = 2
+
+FLOPS = 2 * GRAPHS * NODES * NODES * CHANNELS + 2 * GRAPHS * NODES * FEATURES * CHANNELS
+
+
+def tile_encoder_flows_pb_kernel(tc, flows, x_gcn1, W2, b2, out):
+    nc = tc.nc
+    with ExitStack() as ctx:
+        const = ctx.enter_context(tc.tile_pool(name="const", bufs=1))
+        keep = ctx.enter_context(tc.tile_pool(name="keep", bufs=1))
+        raw_pool = ctx.enter_context(tc.tile_pool(name="raw", bufs=5))
+        grouped_pool = ctx.enter_context(tc.tile_pool(name="grouped", bufs=6))
+        small = ctx.enter_context(tc.tile_pool(name="small", bufs=2))
+        result_pool = ctx.enter_context(tc.tile_pool(name="result", bufs=3))
+        deg_psum = ctx.enter_context(tc.psum_pool(name="deg_psum", bufs=1))
+        work_psum = ctx.enter_context(tc.psum_pool(name="work_psum", bufs=3))
+        acc_psum = ctx.enter_context(tc.psum_pool(name="acc_psum", bufs=4))
+
+        ones = const.tile([P, P], BF16)
+        nc.vector.memset(ones[:], 1.0)
+        identity_f32 = const.tile([P, P], F32)
+        make_identity(nc, identity_f32[:])
+        identity = const.tile([P, P], BF16)
+        nc.vector.tensor_copy(out=identity[:], in_=identity_f32[:])
+        select = const.tile([P, PACK, P // 32, 32], F32)
+        nc.vector.tensor_copy(
+            out=select[:],
+            in_=identity_f32[:].rearrange("p (j t) -> p t j", t=PACK).unsqueeze(2).to_broadcast([P, PACK, P // 32, 32]),
+        )
+        scratch = const.tile([P, 1], F32)
+        nc.vector.memset(scratch[:], 1.0)
+        nc.scalar.sqrt(scratch[:], scratch[:])
+
+        flow_codes = [
+            keep.tile([P, PASSES, NODES], U32, name="flow_codes%d" % g, align_bytes=64)
+            for g in range(GRAPHS)
+        ]
+        flow_scales = [
+            keep.tile([P, PASSES, NODES], U8, name="flow_scales%d" % g, align_bytes=64)
+            for g in range(GRAPHS)
+        ]
+        msg_codes = [
+            keep.tile([P, PASSES, CHANNELS], U32, name="msg_codes%d" % g, align_bytes=64)
+            for g in range(GRAPHS)
+        ]
+        msg_scales = [
+            keep.tile([P, PASSES, CHANNELS], U8, name="msg_scales%d" % g, align_bytes=64)
+            for g in range(GRAPHS)
+        ]
+        x_rows = [keep.tile([P, NODE_TILES, FEATURES], BF16, name="x_rows%d" % g) for g in range(GRAPHS)]
+        x_cols = [keep.tile([P, NODE_TILES, P], BF16, name="x_cols%d" % g) for g in range(GRAPHS)]
+        w2_sb = const.tile([FEATURES, CHANNELS], BF16)
+        bias_row = const.tile([P, CHANNELS], BF16)
+        bias = const.tile([P, CHANNELS], F32)
+
+        raw = {}
+        deg_parts = {}
+        dinv_msg = {}
+        dinv = {}
+
+        def load_rows(g, a):
+            raw[g, a] = raw_pool.tile([P, PACK, NODES], BF16, name="raw")
+            rows = flows[g, a * P * PACK : (a + 1) * P * PACK, :].rearrange("(p t) c -> p t c", t=PACK)
+            for t in range(PACK):
+                nc.sync.dma_start(out=raw[g, a][:, t, :], in_=rows[:, t, :])
+
+        def load_features(g):
+            nc.sync.dma_start(
+                out=x_rows[g][:].rearrange("p (a t) k -> p a t k", t=PACK),
+                in_=x_gcn1[g].rearrange("(a p t) k -> p a t k", p=P, t=PACK),
+            )
+
+        def transpose_features(g):
+            for q in range(NODE_TILES // PACK):
+                turned = work_psum.tile([P, PACK, P], BF16, tag="work")
+                for j in range(PACK):
+                    nc.tensor.transpose(turned[:, j, :], x_rows[g][:, q * PACK + j, :], identity[:])
+                nc.scalar.copy(out=x_cols[g][:, q * PACK : (q + 1) * PACK, :], in_=turned[:])
+
+        def degree_parts(g, a):
+            if a == 0:
+                deg_parts[g] = deg_psum.tile([P, NODE_TILES, NODE_TILES], F32, name="deg_parts")
+            for t in range(PACK):
+                for n in range(NODE_TILES):
+                    nc.tensor.matmul(
+                        out=deg_parts[g][:, n, a * PACK + t : a * PACK + t + 1],
+                        lhsT=raw[g, a][:, t, n * P : (n + 1) * P],
+                        rhs=ones[:, 0:1],
+                        start=True,
+                        stop=True,
+                    )
+
+        def regroup(copy, g, a, u, grouped, first, last):
+            copy(
+                out=grouped[:, first:last, :].rearrange("p (c i) t -> p c t i", i=RUN),
+                in_=raw[g, a][:, :, u * UNIT + first : u * UNIT + last].rearrange(
+                    "p t (c i) -> p c t i", i=RUN
+                ),
+            )
+
+        def regroup_unit(g, a, u):
+            grouped = grouped_pool.tile([P, UNIT, PACK], BF16, name="grouped", align_bytes=64)
+            if VECTOR_COLUMNS[g] > 0:
+                regroup(nc.vector.tensor_copy, g, a, u, grouped, 0, VECTOR_COLUMNS[g])
+            regroup(nc.scalar.copy, g, a, u, grouped, VECTOR_COLUMNS[g], UNIT)
+            return grouped
+
+        def quantise_unit(g, a, u, grouped):
+            cols = slice(u * UNIT, (u + 1) * UNIT)
+            nc.vector.quantize_mx(
+                out=flow_codes[g][:, a, cols].bitcast(FP8X4),
+                scales=flow_scales[g][:, a, cols],
+                in_=grouped[:].rearrange("p c t -> p (c t)"),
+            )
+
+        def normalisers(g):
+            deg = small.tile([P, NODE_TILES], F32, name="deg")
+            nc.vector.tensor_reduce(out=deg[:], in_=deg_parts[g][:], axis=AXIS.X, op=ALU.add)
+            safe = small.tile([P, NODE_TILES], F32, name="safe")
+            nc.vector.scalar_tensor_tensor(
+                out=safe[:], in0=deg[:], scalar=0.0, in1=deg[:], op0=ALU.is_le, op1=ALU.add
+            )
+            root = small.tile([P, NODE_TILES], F32, name="root")
+            nc.scalar.sqrt(root[:], safe[:])
+            inverse = small.tile([P, NODE_TILES], F32, name="inverse")
+            nc.vector.reciprocal(inverse[:], root[:])
+            dinv[g] = small.tile([P, NODE_TILES], F32, name="dinv")
+            nc.vector.scalar_tensor_tensor(
+                out=dinv[g][:], in0=deg[:], scalar=0.0, in1=inverse[:], op0=ALU.is_gt, op1=ALU.mult
+            )
+            picked = work_psum.tile([P, PACK, NODE_TILES], F32, tag="work")
+            for t in range(PACK):
+                nc.tensor.matmul(
+                    out=picked[:, t, :],
+                    lhsT=select[:, t, :, :].rearrange("p q j -> p (q j)"),
+                    rhs=dinv[g][:],
+                    start=True,
+                    stop=True,
+                )
+            dinv_msg[g] = small.tile([P, NODE_TILES], F32, name="dinv_msg")
+            for q in range(P // 32):
+                part = slice(32 * q, 32 * (q + 1))
+                nc.vector.tensor_copy(
+                    out=dinv_msg[g][part, :].rearrange("p (a t) -> p a t", t=PACK),
+                    in_=picked[part, :, q : NODE_TILES : 4].rearrange("p t a -> p a t"),
+                )
+
+        def messages(g):
+            grouped_msg = keep.tile([P, PASSES, CHANNELS, PACK], BF16, name="grouped_msg", align_bytes=64)
+            for a in range(PASSES):
+                for h in range(CHANNELS // HALF):
+                    xw = work_psum.tile([P, PACK, HALF], F32, tag="work")
+                    for t in range(PACK):
+                        nc.tensor.matmul(
+                            out=xw[:, t, :],
+                            lhsT=x_cols[g][:, a * PACK + t, :],
+                            rhs=w2_sb[:, h * HALF : (h + 1) * HALF],
+                            start=True,
+                            stop=True,
+                        )
+                    nc.vector.tensor_tensor(
+                        out=grouped_msg[:, a, h * HALF : (h + 1) * HALF, :],
+                        in0=xw[:].rearrange("p t i -> p i t"),
+                        in1=dinv_msg[g][:, a * PACK : (a + 1) * PACK].unsqueeze(1).to_broadcast([P, HALF, PACK]),
+                        op=ALU.mult,
+                    )
+                nc.vector.quantize_mx(
+                    out=msg_codes[g][:, a, :].bitcast(FP8X4),
+                    scales=msg_scales[g][:, a, :],
+                    in_=grouped_msg[:, a, :, :].rearrange("p i t -> p (i t)"),
+                )
+
+        acc = {}
+        results = {}
+
+        def multiply(g, n):
+            acc[g, n] = acc_psum.tile([P, CHANNELS], F32, name="acc")
+            for a in range(PASSES):
+                nc.tensor.matmul_mx(
+                    out=acc[g, n][:],
+                    lhsT=flow_codes[g][:, a, n * P : (n + 1) * P].bitcast(FP8X4),
+                    lhsT_scale=flow_scales[g][:, a, n * P : (n + 1) * P],
+                    rhs=msg_codes[g][:, a, :].bitcast(FP8X4),
+                    rhs_scale=msg_scales[g][:, a, :],
+                    start=(a == 0),
+                    stop=(a == PASSES - 1),
+                )
+
+        def finish(g, n):
+            j = n % STORE_TILES
+            if j == 0:
+                results[g] = result_pool.tile([P, STORE_TILES, CHANNELS], F32, name="result")
+            nc.vector.scalar_tensor_tensor(
+                out=results[g][:, j, :],
+                in0=acc[g, n][:],
+                scalar=dinv[g][:, n : n + 1],
+                in1=bias[:],
+                op0=ALU.mult,
+                op1=ALU.add,
+            )
+            if j == STORE_TILES - 1:
+                first = (n - j) * P
+                nc.sync.dma_start(
+                    out=out[g, first : first + STORE_TILES * P, :].rearrange("(j p) i -> p j i", p=P),
+                    in_=results[g][:],
+                )
+
+        load_rows(0, 0)
+        nc.sync.dma_start(out=w2_sb[:], in_=W2)
+        nc.vector.memset(bias_row[:], 0.0)
+        nc.sync.dma_start(out=bias_row[0:1, :], in_=b2.unsqueeze(0))
+        load_features(0)
+        for a in range(1, PASSES):
+            load_rows(0, a)
+        load_rows(1, 0)
+
+        waiting = []
+
+        def next_unit(g, a, u):
+            grouped = regroup_unit(g, a, u)
+            if waiting:
+                quantise_unit(*waiting.pop())
+            waiting.append((g, a, u, grouped))
+
+        for a in range(PASSES):
+            with tc.high_priority():
+                degree_parts(0, a)
+            for u in range(UNITS):
+                next_unit(0, a, u)
+            if a + 1 < PASSES:
+                load_rows(1, a + 1)
+            if a == 0:
+                spread = work_psum.tile([P, CHANNELS], F32, tag="work")
+                nc.tensor.matmul(out=spread[:], lhsT=ones[:], rhs=bias_row[:], start=True, stop=True)
+                nc.vector.tensor_copy(out=bias[:], in_=spread[:])
+                transpose_features(0)
+        load_features(1)
+        with tc.high_priority():
+            normalisers(0)
+            messages(0)
+
+        for a in range(PASSES // 2):
+            with tc.high_priority():
+                degree_parts(1, a)
+            for u in range(UNITS):
+                next_unit(1, a, u)
+
+        with tc.high_priority():
+            for a in range(PASSES // 2, PASSES):
+                degree_parts(1, a)
+            transpose_features(1)
+            normalisers(1)
+            messages(1)
+
+        for n in range(AHEAD):
+            multiply(0, n)
+        for n in range(NODE_TILES):
+            if n + AHEAD < NODE_TILES:
+                multiply(0, n + AHEAD)
+            finish(0, n)
+
+        tiles_of_unit = UNIT // P
+        for u in range(UNITS + 2):
+            if u < UNITS:
+                next_unit(1, PASSES - 2, u)
+                next_unit(1, PASSES - 1, u)
+            if u == UNITS:
+                quantise_unit(*waiting.pop())
+            if 2 <= u:
+                for n in range((u - 2) * tiles_of_unit, (u - 1) * tiles_of_unit):
+                    finish(1, n)
+            if 1 <= u <= UNITS:
+                for n in range((u - 1) * tiles_of_unit, u * tiles_of_unit):
+                    multiply(1, n)

@@ -13,6 +13,8 @@ AXIS = mybir.AxisListType
 
 P = 128
 PACK = 4
+QUAD = 32
+QUADS = P // QUAD
 GRAPHS = 2
 NODES = 2048
 FEATURES = 128
@@ -21,11 +23,12 @@ PASSES = NODES // (P * PACK)
 NODE_TILES = NODES // P
 UNIT = 512
 UNITS = NODES // UNIT
-VECTOR_COLUMNS = (256, 64)
+UNIT_TILES = UNIT // P
 RUN = 4
 HALF = CHANNELS // 2
-STORE_TILES = 2
-AHEAD = 2
+PAIR = 2
+PAIRS = NODE_TILES // PAIR
+RAW_BUFS = {1: 2, 2: 9}
 
 FLOPS = 2 * GRAPHS * NODES * NODES * CHANNELS + 2 * GRAPHS * NODES * FEATURES * CHANNELS
 
@@ -35,28 +38,14 @@ def tile_encoder_flows_pb_kernel(tc, flows, x_gcn1, W2, b2, out):
     with ExitStack() as ctx:
         const = ctx.enter_context(tc.tile_pool(name="const", bufs=1))
         keep = ctx.enter_context(tc.tile_pool(name="keep", bufs=1))
-        raw_pool = ctx.enter_context(tc.tile_pool(name="raw", bufs=5))
-        grouped_pool = ctx.enter_context(tc.tile_pool(name="grouped", bufs=6))
+        raw_pool = ctx.enter_context(tc.tile_pool(name="raw", bufs=9))
+        grouped_pool = ctx.enter_context(tc.tile_pool(name="grouped", bufs=7))
         small = ctx.enter_context(tc.tile_pool(name="small", bufs=2))
         result_pool = ctx.enter_context(tc.tile_pool(name="result", bufs=3))
         deg_psum = ctx.enter_context(tc.psum_pool(name="deg_psum", bufs=1))
-        work_psum = ctx.enter_context(tc.psum_pool(name="work_psum", bufs=3))
-        acc_psum = ctx.enter_context(tc.psum_pool(name="acc_psum", bufs=4))
-
-        ones = const.tile([P, P], BF16)
-        nc.vector.memset(ones[:], 1.0)
-        identity_f32 = const.tile([P, P], F32)
-        make_identity(nc, identity_f32[:])
-        identity = const.tile([P, P], BF16)
-        nc.vector.tensor_copy(out=identity[:], in_=identity_f32[:])
-        select = const.tile([P, PACK, P // 32, 32], F32)
-        nc.vector.tensor_copy(
-            out=select[:],
-            in_=identity_f32[:].rearrange("p (j t) -> p t j", t=PACK).unsqueeze(2).to_broadcast([P, PACK, P // 32, 32]),
-        )
-        scratch = const.tile([P, 1], F32)
-        nc.vector.memset(scratch[:], 1.0)
-        nc.scalar.sqrt(scratch[:], scratch[:])
+        work_psum = ctx.enter_context(tc.psum_pool(name="work_psum", bufs=4))
+        acc_psum = ctx.enter_context(tc.psum_pool(name="acc_psum", bufs=3))
+        ctx.enter_context(tc.manual_schedule())
 
         flow_codes = [
             keep.tile([P, PASSES, NODES], U32, name="flow_codes%d" % g, align_bytes=64)
@@ -74,228 +63,397 @@ def tile_encoder_flows_pb_kernel(tc, flows, x_gcn1, W2, b2, out):
             keep.tile([P, PASSES, CHANNELS], U8, name="msg_scales%d" % g, align_bytes=64)
             for g in range(GRAPHS)
         ]
-        x_rows = [keep.tile([P, NODE_TILES, FEATURES], BF16, name="x_rows%d" % g) for g in range(GRAPHS)]
-        x_cols = [keep.tile([P, NODE_TILES, P], BF16, name="x_cols%d" % g) for g in range(GRAPHS)]
         w2_sb = const.tile([FEATURES, CHANNELS], BF16)
         bias_row = const.tile([P, CHANNELS], BF16)
         bias = const.tile([P, CHANNELS], F32)
+        deg_parts = deg_psum.tile([P, GRAPHS, NODE_TILES, PASSES], F32)
 
+        x_rows = {}
+        x_cols = {}
         raw = {}
-        deg_parts = {}
-        dinv_msg = {}
+        grouped = {}
+        deg = {}
+        root = {}
+        dinv_spread = {}
         dinv = {}
+        dinv_msg = {}
+        picked = {}
+        grouped_msg = {}
+        xw = {}
+        acc = {}
 
-        def load_rows(g, a):
-            raw[g, a] = raw_pool.tile([P, PACK, NODES], BF16, name="raw")
+        def load_rows(g, a, first, count):
+            chunk = raw_pool.tile([P, PACK, count * UNIT], BF16, name="raw%d" % count, bufs=RAW_BUFS[count])
             rows = flows[g, a * P * PACK : (a + 1) * P * PACK, :].rearrange("(p t) c -> p t c", t=PACK)
-            for t in range(PACK):
-                nc.sync.dma_start(out=raw[g, a][:, t, :], in_=rows[:, t, :])
+            nc.sync.dma_start(out=chunk[:], in_=rows[:, :, first * UNIT : (first + count) * UNIT])
+            for i in range(count):
+                raw[g, a, first + i] = chunk[:, :, i * UNIT : (i + 1) * UNIT]
 
         def load_features(g):
+            x_rows[g] = keep.tile([P, NODE_TILES, FEATURES], BF16, name="x_rows%d" % g)
             nc.sync.dma_start(
                 out=x_rows[g][:].rearrange("p (a t) k -> p a t k", t=PACK),
                 in_=x_gcn1[g].rearrange("(a p t) k -> p a t k", p=P, t=PACK),
             )
 
-        def transpose_features(g):
-            for q in range(NODE_TILES // PACK):
-                turned = work_psum.tile([P, PACK, P], BF16, tag="work")
-                for j in range(PACK):
-                    nc.tensor.transpose(turned[:, j, :], x_rows[g][:, q * PACK + j, :], identity[:])
-                nc.scalar.copy(out=x_cols[g][:, q * PACK : (q + 1) * PACK, :], in_=turned[:])
-
-        def degree_parts(g, a):
+        def transpose_features(g, a):
             if a == 0:
-                deg_parts[g] = deg_psum.tile([P, NODE_TILES, NODE_TILES], F32, name="deg_parts")
+                x_cols[g] = keep.tile([P, NODE_TILES, P], BF16, name="x_cols%d" % g)
+            turned = work_psum.tile([P, PACK, P], BF16, tag="work")
             for t in range(PACK):
-                for n in range(NODE_TILES):
+                nc.tensor.transpose(turned[:, t, :], x_rows[g][:, a * PACK + t, :], identity[:])
+            nc.scalar.copy(out=x_cols[g][:, a * PACK : (a + 1) * PACK, :], in_=turned[:])
+
+        def degree_unit(g, a, u):
+            for n in range(u * UNIT_TILES, (u + 1) * UNIT_TILES):
+                for t in range(PACK):
                     nc.tensor.matmul(
-                        out=deg_parts[g][:, n, a * PACK + t : a * PACK + t + 1],
-                        lhsT=raw[g, a][:, t, n * P : (n + 1) * P],
+                        out=deg_parts[:, g, n, a : a + 1],
+                        lhsT=raw[g, a, u][:, t, (n % UNIT_TILES) * P : (n % UNIT_TILES + 1) * P],
                         rhs=ones[:, 0:1],
-                        start=True,
-                        stop=True,
+                        start=(t == 0),
+                        stop=(t == PACK - 1),
                     )
 
-        def regroup(copy, g, a, u, grouped, first, last):
+        def regroup(copy, g, a, u, first, last):
             copy(
-                out=grouped[:, first:last, :].rearrange("p (c i) t -> p c t i", i=RUN),
-                in_=raw[g, a][:, :, u * UNIT + first : u * UNIT + last].rearrange(
-                    "p t (c i) -> p c t i", i=RUN
-                ),
+                out=grouped[g, a, u][:, first:last, :].rearrange("p (c i) t -> p c t i", i=RUN),
+                in_=raw[g, a, u][:, :, first:last].rearrange("p t (c i) -> p c t i", i=RUN),
             )
 
-        def regroup_unit(g, a, u):
-            grouped = grouped_pool.tile([P, UNIT, PACK], BF16, name="grouped", align_bytes=64)
-            if VECTOR_COLUMNS[g] > 0:
-                regroup(nc.vector.tensor_copy, g, a, u, grouped, 0, VECTOR_COLUMNS[g])
-            regroup(nc.scalar.copy, g, a, u, grouped, VECTOR_COLUMNS[g], UNIT)
-            return grouped
+        def open_unit(g, a, u):
+            if (g, a, u) not in grouped:
+                grouped[g, a, u] = grouped_pool.tile([P, UNIT, PACK], BF16, name="grouped", align_bytes=64)
 
-        def quantise_unit(g, a, u, grouped):
+        def regroup_unit(g, a, u, vector_columns):
+            open_unit(g, a, u)
+            regroup(nc.scalar.copy, g, a, u, vector_columns, UNIT)
+
+        def regroup_vector(g, a, u, vector_columns):
+            if vector_columns > 0:
+                open_unit(g, a, u)
+                regroup(nc.vector.tensor_copy, g, a, u, 0, vector_columns)
+
+        def quantise_unit(g, a, u):
             cols = slice(u * UNIT, (u + 1) * UNIT)
             nc.vector.quantize_mx(
                 out=flow_codes[g][:, a, cols].bitcast(FP8X4),
                 scales=flow_scales[g][:, a, cols],
-                in_=grouped[:].rearrange("p c t -> p (c t)"),
+                in_=grouped[g, a, u][:].rearrange("p c t -> p (c t)"),
             )
 
-        def normalisers(g):
-            deg = small.tile([P, NODE_TILES], F32, name="deg")
-            nc.vector.tensor_reduce(out=deg[:], in_=deg_parts[g][:], axis=AXIS.X, op=ALU.add)
+        def degrees(g):
+            deg[g] = small.tile([P, NODE_TILES], F32, name="deg")
+            nc.vector.tensor_reduce(out=deg[g][:], in_=deg_parts[:, g, :, :], axis=AXIS.X, op=ALU.add)
+
+        def roots(g):
             safe = small.tile([P, NODE_TILES], F32, name="safe")
             nc.vector.scalar_tensor_tensor(
-                out=safe[:], in0=deg[:], scalar=0.0, in1=deg[:], op0=ALU.is_le, op1=ALU.add
+                out=safe[:], in0=deg[g][:], scalar=0.0, in1=deg[g][:], op0=ALU.is_le, op1=ALU.add
             )
-            root = small.tile([P, NODE_TILES], F32, name="root")
-            nc.scalar.sqrt(root[:], safe[:])
+            root[g] = small.tile([P, NODE_TILES], F32, name="root")
+            nc.scalar.sqrt(root[g][:], safe[:])
+
+        def inverses(g):
             inverse = small.tile([P, NODE_TILES], F32, name="inverse")
-            nc.vector.reciprocal(inverse[:], root[:])
+            nc.vector.reciprocal(inverse[:], root[g][:])
             dinv[g] = small.tile([P, NODE_TILES], F32, name="dinv")
             nc.vector.scalar_tensor_tensor(
-                out=dinv[g][:], in0=deg[:], scalar=0.0, in1=inverse[:], op0=ALU.is_gt, op1=ALU.mult
+                out=dinv[g][:], in0=deg[g][:], scalar=0.0, in1=inverse[:], op0=ALU.is_gt, op1=ALU.mult
             )
-            picked = work_psum.tile([P, PACK, NODE_TILES], F32, tag="work")
-            for t in range(PACK):
-                nc.tensor.matmul(
-                    out=picked[:, t, :],
-                    lhsT=select[:, t, :, :].rearrange("p q j -> p (q j)"),
-                    rhs=dinv[g][:],
-                    start=True,
-                    stop=True,
-                )
+            dinv_spread[g] = small.tile([P, NODE_TILES, PACK], F32, name="dinv_spread")
+            nc.vector.tensor_tensor(
+                out=dinv_spread[g][:],
+                in0=dinv[g][:].unsqueeze(2).to_broadcast([P, NODE_TILES, PACK]),
+                in1=residue[:].unsqueeze(1).to_broadcast([P, NODE_TILES, PACK]),
+                op=ALU.mult,
+            )
+
+        def pick_inverses(g):
+            picked[g] = work_psum.tile([P, NODE_TILES, PACK], F32, name="picked", tag="work")
+            nc.tensor.matmul(
+                out=picked[g][:].rearrange("p n t -> p (n t)"),
+                lhsT=fours[:].rearrange("p q j -> p (q j)"),
+                rhs=dinv_spread[g][:].rearrange("p n t -> p (n t)"),
+                start=True,
+                stop=True,
+            )
+
+        def message_inverses(g):
             dinv_msg[g] = small.tile([P, NODE_TILES], F32, name="dinv_msg")
-            for q in range(P // 32):
-                part = slice(32 * q, 32 * (q + 1))
+            for q in range(QUADS):
+                part = slice(QUAD * q, QUAD * (q + 1))
                 nc.vector.tensor_copy(
                     out=dinv_msg[g][part, :].rearrange("p (a t) -> p a t", t=PACK),
-                    in_=picked[part, :, q : NODE_TILES : 4].rearrange("p t a -> p a t"),
+                    in_=picked[g][part, q : NODE_TILES : QUADS, :],
                 )
 
-        def messages(g):
-            grouped_msg = keep.tile([P, PASSES, CHANNELS, PACK], BF16, name="grouped_msg", align_bytes=64)
-            for a in range(PASSES):
-                for h in range(CHANNELS // HALF):
-                    xw = work_psum.tile([P, PACK, HALF], F32, tag="work")
-                    for t in range(PACK):
-                        nc.tensor.matmul(
-                            out=xw[:, t, :],
-                            lhsT=x_cols[g][:, a * PACK + t, :],
-                            rhs=w2_sb[:, h * HALF : (h + 1) * HALF],
-                            start=True,
-                            stop=True,
-                        )
-                    nc.vector.tensor_tensor(
-                        out=grouped_msg[:, a, h * HALF : (h + 1) * HALF, :],
-                        in0=xw[:].rearrange("p t i -> p i t"),
-                        in1=dinv_msg[g][:, a * PACK : (a + 1) * PACK].unsqueeze(1).to_broadcast([P, HALF, PACK]),
-                        op=ALU.mult,
+        def features_times_weights(g, a):
+            for h in range(CHANNELS // HALF):
+                xw[g, a, h] = work_psum.tile([P, PACK, HALF], F32, name="xw", tag="work")
+                for t in range(PACK):
+                    nc.tensor.matmul(
+                        out=xw[g, a, h][:, t, :],
+                        lhsT=x_cols[g][:, a * PACK + t, :],
+                        rhs=w2_sb[:, h * HALF : (h + 1) * HALF],
+                        start=True,
+                        stop=True,
                     )
-                nc.vector.quantize_mx(
-                    out=msg_codes[g][:, a, :].bitcast(FP8X4),
-                    scales=msg_scales[g][:, a, :],
-                    in_=grouped_msg[:, a, :, :].rearrange("p i t -> p (i t)"),
+
+        def scale_messages(g, a):
+            if a == 0:
+                grouped_msg[g] = keep.tile([P, PASSES, CHANNELS, PACK], BF16, name="grouped_msg", align_bytes=64)
+            for h in range(CHANNELS // HALF):
+                nc.vector.tensor_tensor(
+                    out=grouped_msg[g][:, a, h * HALF : (h + 1) * HALF, :],
+                    in0=xw[g, a, h][:].rearrange("p t i -> p i t"),
+                    in1=dinv_msg[g][:, a * PACK : (a + 1) * PACK].unsqueeze(1).to_broadcast([P, HALF, PACK]),
+                    op=ALU.mult,
                 )
 
-        acc = {}
-        results = {}
+        def quantise_messages(g, a):
+            nc.vector.quantize_mx(
+                out=msg_codes[g][:, a, :].bitcast(FP8X4),
+                scales=msg_scales[g][:, a, :],
+                in_=grouped_msg[g][:, a, :, :].rearrange("p i t -> p (i t)"),
+            )
 
-        def multiply(g, n):
-            acc[g, n] = acc_psum.tile([P, CHANNELS], F32, name="acc")
-            for a in range(PASSES):
+        def product_passes(g, n, passes):
+            rows = slice(n * P, (n + 1) * P)
+            for a in passes:
                 nc.tensor.matmul_mx(
-                    out=acc[g, n][:],
-                    lhsT=flow_codes[g][:, a, n * P : (n + 1) * P].bitcast(FP8X4),
-                    lhsT_scale=flow_scales[g][:, a, n * P : (n + 1) * P],
+                    out=acc[g, n],
+                    lhsT=flow_codes[g][:, a, rows].bitcast(FP8X4),
+                    lhsT_scale=flow_scales[g][:, a, rows],
                     rhs=msg_codes[g][:, a, :].bitcast(FP8X4),
                     rhs_scale=msg_scales[g][:, a, :],
                     start=(a == 0),
                     stop=(a == PASSES - 1),
                 )
 
-        def finish(g, n):
-            j = n % STORE_TILES
-            if j == 0:
-                results[g] = result_pool.tile([P, STORE_TILES, CHANNELS], F32, name="result")
-            nc.vector.scalar_tensor_tensor(
-                out=results[g][:, j, :],
-                in0=acc[g, n][:],
-                scalar=dinv[g][:, n : n + 1],
-                in1=bias[:],
-                op0=ALU.mult,
-                op1=ALU.add,
-            )
-            if j == STORE_TILES - 1:
-                first = (n - j) * P
-                nc.sync.dma_start(
-                    out=out[g, first : first + STORE_TILES * P, :].rearrange("(j p) i -> p j i", p=P),
-                    in_=results[g][:],
-                )
+        def multiply(g, j):
+            bank = acc_psum.tile([P, PAIR, CHANNELS], F32, name="bank")
+            for i in range(PAIR):
+                acc[g, PAIR * j + i] = bank[:, i, :]
+                product_passes(g, PAIR * j + i, range(PASSES))
 
-        load_rows(0, 0)
-        nc.sync.dma_start(out=w2_sb[:], in_=W2)
+        def begin_last(n):
+            bank = work_psum.tile([P, CHANNELS], F32, name="last", tag="work")
+            acc[1, n] = bank[:]
+            product_passes(1, n, range(PASSES - 1))
+
+        def end_last(n):
+            product_passes(1, n, [PASSES - 1])
+
+        def finish(g, j):
+            result = result_pool.tile([P, PAIR, CHANNELS], F32, name="result")
+            for i in range(PAIR):
+                n = j * PAIR + i
+                nc.vector.scalar_tensor_tensor(
+                    out=result[:, i, :],
+                    in0=acc[g, n],
+                    scalar=dinv[g][:, n : n + 1],
+                    in1=bias[:],
+                    op0=ALU.mult,
+                    op1=ALU.add,
+                )
+            nc.sync.dma_start(
+                out=out[g, j * PAIR * P : (j + 1) * PAIR * P, :].rearrange("(i p) c -> p i c", p=P),
+                in_=result[:],
+            )
+
+        load_rows(0, 0, 0, 1)
+        load_rows(0, 0, 1, 1)
+        load_rows(0, 0, 2, 2)
+        ones = const.tile([P, P], BF16)
+        nc.vector.memset(ones[:], 1.0)
+        scratch = const.tile([P, 1], F32)
+        nc.vector.memset(scratch[:], 1.0)
+        nc.scalar.sqrt(scratch[:], scratch[:])
         nc.vector.memset(bias_row[:], 0.0)
+        identity_f32 = const.tile([P, P], F32)
+        make_identity(nc, identity_f32[:])
+        identity = const.tile([P, P], BF16)
+        nc.vector.tensor_copy(out=identity[:], in_=identity_f32[:])
+        four = const.tile([P, QUAD], F32)
+        nc.vector.tensor_reduce(
+            out=four[:], in_=identity_f32[:].rearrange("p (j t) -> p j t", t=PACK), axis=AXIS.X, op=ALU.add
+        )
+        fours = const.tile([P, QUADS, QUAD], F32)
+        nc.vector.tensor_copy(out=fours[:], in_=four[:].unsqueeze(1).to_broadcast([P, QUADS, QUAD]))
+        residue = const.tile([P, PACK], F32)
+        nc.vector.tensor_reduce(
+            out=residue[:], in_=identity_f32[:].rearrange("p (j t) -> p t j", t=PACK), axis=AXIS.X, op=ALU.add
+        )
+        load_rows(0, 1, 0, 2)
+        load_rows(0, 1, 2, 2)
+        nc.sync.dma_start(out=w2_sb[:], in_=W2)
         nc.sync.dma_start(out=bias_row[0:1, :], in_=b2.unsqueeze(0))
         load_features(0)
-        for a in range(1, PASSES):
-            load_rows(0, a)
-        load_rows(1, 0)
+        arrivals = [(g, a, h) for g in range(GRAPHS) for a in range(PASSES) for h in range(UNITS // 2)]
+        for g, a, h in arrivals[4:10]:
+            load_rows(g, a, 2 * h, 2)
+            if (g, a, h) == (0, PASSES - 1, 1):
+                load_features(1)
+        late_loads = arrivals[10:]
 
         waiting = []
 
-        def next_unit(g, a, u):
-            grouped = regroup_unit(g, a, u)
+        def quantise_waiting():
             if waiting:
-                quantise_unit(*waiting.pop())
-            waiting.append((g, a, u, grouped))
-
-        for a in range(PASSES):
-            with tc.high_priority():
-                degree_parts(0, a)
-            for u in range(UNITS):
-                next_unit(0, a, u)
-            if a + 1 < PASSES:
-                load_rows(1, a + 1)
-            if a == 0:
+                quantise_unit(*waiting.pop(0))
+        for k in range(PASSES * UNITS):
+            a, u = divmod(k, UNITS)
+            share = ([272,272,272,272,272,272,272,272,272,272,272,272,272,272,272,272])[k]
+            degree_unit(0, a, u)
+            regroup_unit(0, a, u, share)
+            if k == 15:
+                degrees(0)
+            regroup_vector(0, a, u, share)
+            if len(waiting) >= 1:
+                quantise_waiting()
+            waiting.append((0, a, u))
+            if k >= 3 and u % 2 == 1 and late_loads:
+                g, aa, h = late_loads.pop(0)
+                load_rows(g, aa, 2 * h, 2)
+            if k == 6:
                 spread = work_psum.tile([P, CHANNELS], F32, tag="work")
                 nc.tensor.matmul(out=spread[:], lhsT=ones[:], rhs=bias_row[:], start=True, stop=True)
                 nc.vector.tensor_copy(out=bias[:], in_=spread[:])
-                transpose_features(0)
-        load_features(1)
-        with tc.high_priority():
-            normalisers(0)
-            messages(0)
-
-        for a in range(PASSES // 2):
-            with tc.high_priority():
-                degree_parts(1, a)
-            for u in range(UNITS):
-                next_unit(1, a, u)
-
-        with tc.high_priority():
-            for a in range(PASSES // 2, PASSES):
-                degree_parts(1, a)
-            transpose_features(1)
-            normalisers(1)
-            messages(1)
-
-        for n in range(AHEAD):
-            multiply(0, n)
-        for n in range(NODE_TILES):
-            if n + AHEAD < NODE_TILES:
-                multiply(0, n + AHEAD)
-            finish(0, n)
-
-        tiles_of_unit = UNIT // P
-        for u in range(UNITS + 2):
-            if u < UNITS:
-                next_unit(1, PASSES - 2, u)
-                next_unit(1, PASSES - 1, u)
-            if u == UNITS:
-                quantise_unit(*waiting.pop())
-            if 2 <= u:
-                for n in range((u - 2) * tiles_of_unit, (u - 1) * tiles_of_unit):
-                    finish(1, n)
-            if 1 <= u <= UNITS:
-                for n in range((u - 1) * tiles_of_unit, u * tiles_of_unit):
-                    multiply(1, n)
+            if 8 <= k < 8 + PASSES:
+                transpose_features(0, k - 8)
+        features_times_weights(0, 0)
+        roots(0)
+        transpose_features(1, 0)
+        transpose_features(1, 1)
+        transpose_features(1, 2)
+        transpose_features(1, 3)
+        inverses(0)
+        pick_inverses(0)
+        degree_unit(1, 0, 0)
+        regroup_unit(1, 0,0, 192)
+        regroup_vector(1, 0,0, 192)
+        quantise_waiting()
+        degree_unit(1, 0, 1)
+        features_times_weights(0, 0)
+        regroup_vector(1, 0,1, 192)
+        regroup_unit(1, 0,1, 192)
+        degree_unit(1, 0, 2)
+        message_inverses(0)
+        scale_messages(0, 0)
+        features_times_weights(0, 1)
+        degree_unit(1, 0, 3)
+        scale_messages(0, 1)
+        features_times_weights(0, 2)
+        degree_unit(1, 1, 0)
+        regroup_unit(1, 0,2, 0)
+        scale_messages(0, 2)
+        features_times_weights(0, 3)
+        degree_unit(1, 1, 1)
+        scale_messages(0, 3)
+        quantise_messages(0, 0)
+        quantise_messages(0, 1)
+        degree_unit(1, 1, 2)
+        degree_unit(1, 1, 3)
+        quantise_messages(0, 2)
+        quantise_messages(0, 3)
+        degree_unit(1, 2, 0)
+        degree_unit(1, 2, 1)
+        multiply(0, 0)
+        quantise_unit(1, 0,0)
+        quantise_unit(1, 0,1)
+        regroup_unit(1, 0,3, 0)
+        degree_unit(1, 2, 2)
+        degree_unit(1, 2, 3)
+        multiply(0, 1)
+        quantise_unit(1, 0,2)
+        regroup_unit(1, 1,0, 96)
+        finish(0, 0)
+        regroup_vector(1, 1,0, 96)
+        regroup_vector(1, 1,1, 96)
+        degree_unit(1, 3, 0)
+        degree_unit(1, 3, 1)
+        quantise_unit(1, 0,3)
+        regroup_unit(1, 1,1, 96)
+        finish(0, 1)
+        features_times_weights(1, 0)
+        degree_unit(1, 3, 2)
+        degree_unit(1, 3, 3)
+        multiply(0, 2)
+        regroup_vector(1, 1,2, 96)
+        regroup_vector(1, 1,3, 96)
+        quantise_unit(1, 1,0)
+        regroup_unit(1, 1,2, 96)
+        finish(0, 2)
+        degrees(1)
+        roots(1)
+        multiply(0, 3)
+        quantise_unit(1, 1,1)
+        regroup_unit(1, 1,3, 96)
+        inverses(1)
+        pick_inverses(1)
+        finish(0, 3)
+        multiply(0, 4)
+        quantise_unit(1, 1,2)
+        regroup_unit(1, 2,0, 0)
+        finish(0, 4)
+        message_inverses(1)
+        scale_messages(1, 0)
+        features_times_weights(1, 1)
+        multiply(0, 5)
+        scale_messages(1, 1)
+        features_times_weights(1, 2)
+        scale_messages(1, 2)
+        features_times_weights(1, 3)
+        multiply(0, 6)
+        scale_messages(1, 3)
+        quantise_messages(1, 0)
+        quantise_messages(1, 1)
+        quantise_messages(1, 2)
+        quantise_messages(1, 3)
+        quantise_unit(1, 1,3)
+        regroup_unit(1, 3,0, 0)
+        quantise_unit(1, 2,0)
+        regroup_unit(1, 2,1, 0)
+        quantise_unit(1, 3,0)
+        regroup_unit(1, 3,1, 0)
+        multiply(0, 7)
+        quantise_unit(1, 2,1)
+        regroup_unit(1, 2,2, 48)
+        finish(0, 5)
+        multiply(1, 0)
+        multiply(1, 1)
+        quantise_unit(1, 3,1)
+        regroup_unit(1, 3,2, 48)
+        finish(0, 6)
+        finish(0, 7)
+        multiply(1, 2)
+        multiply(1, 3)
+        regroup_vector(1, 2,2, 48)
+        quantise_unit(1, 2,2)
+        regroup_unit(1, 2,3, 48)
+        finish(1, 0)
+        finish(1, 1)
+        regroup_vector(1, 3,2, 48)
+        quantise_unit(1, 3,2)
+        regroup_unit(1, 3,3, 48)
+        multiply(1, 4)
+        finish(1, 2)
+        multiply(1, 5)
+        finish(1, 3)
+        regroup_vector(1, 2,3, 48)
+        quantise_unit(1, 2,3)
+        begin_last(12)
+        begin_last(13)
+        begin_last(14)
+        begin_last(15)
+        finish(1, 4)
+        finish(1, 5)
+        regroup_vector(1, 3,3, 48)
+        quantise_unit(1, 3,3)
+        end_last(12)
+        end_last(13)
+        finish(1, 6)
+        end_last(14)
+        end_last(15)
+        finish(1, 7)

@@ -28,7 +28,10 @@ RUN = 4
 HALF = CHANNELS // 2
 PAIR = 2
 PAIRS = NODE_TILES // PAIR
-RAW_BUFS = {1: 2, 2: 9}
+DEG_PARTS = (PASSES, 2 * PASSES - 1)
+COPIES = (2, 24)
+DEG_COLUMNS = [DEG_PARTS[g] * NODE_TILES + COPIES[g] for g in range(GRAPHS)]
+RAW_BUFS = {1: 2, 2: 4, 4: 3}
 
 FLOPS = 2 * GRAPHS * NODES * NODES * CHANNELS + 2 * GRAPHS * NODES * FEATURES * CHANNELS
 
@@ -39,7 +42,7 @@ def tile_encoder_flows_pb_kernel(tc, flows, x_gcn1, W2, b2, out):
         const = ctx.enter_context(tc.tile_pool(name="const", bufs=1))
         keep = ctx.enter_context(tc.tile_pool(name="keep", bufs=1))
         raw_pool = ctx.enter_context(tc.tile_pool(name="raw", bufs=9))
-        grouped_pool = ctx.enter_context(tc.tile_pool(name="grouped", bufs=7))
+        grouped_pool = ctx.enter_context(tc.tile_pool(name="grouped", bufs=6))
         small = ctx.enter_context(tc.tile_pool(name="small", bufs=2))
         result_pool = ctx.enter_context(tc.tile_pool(name="result", bufs=3))
         deg_psum = ctx.enter_context(tc.psum_pool(name="deg_psum", bufs=1))
@@ -66,7 +69,8 @@ def tile_encoder_flows_pb_kernel(tc, flows, x_gcn1, W2, b2, out):
         w2_sb = const.tile([FEATURES, CHANNELS], BF16)
         bias_row = const.tile([P, CHANNELS], BF16)
         bias = const.tile([P, CHANNELS], F32)
-        deg_parts = deg_psum.tile([P, GRAPHS, NODE_TILES, PASSES], F32)
+        deg_bank = deg_psum.tile([P, DEG_COLUMNS[0] + DEG_COLUMNS[1]], F32)
+        deg_parts = [deg_bank[:, : DEG_COLUMNS[0]], deg_bank[:, DEG_COLUMNS[0] :]]
 
         x_rows = {}
         x_cols = {}
@@ -85,7 +89,11 @@ def tile_encoder_flows_pb_kernel(tc, flows, x_gcn1, W2, b2, out):
         def load_rows(g, a, first, count):
             chunk = raw_pool.tile([P, PACK, count * UNIT], BF16, name="raw%d" % count, bufs=RAW_BUFS[count])
             rows = flows[g, a * P * PACK : (a + 1) * P * PACK, :].rearrange("(p t) c -> p t c", t=PACK)
-            nc.sync.dma_start(out=chunk[:], in_=rows[:, :, first * UNIT : (first + count) * UNIT])
+            if count == UNITS:
+                for t in range(0, PACK, 2):
+                    nc.sync.dma_start(out=chunk[:, t : t + 2, :], in_=rows[:, t : t + 2, :])
+            else:
+                nc.sync.dma_start(out=chunk[:], in_=rows[:, :, first * UNIT : (first + count) * UNIT])
             for i in range(count):
                 raw[g, a, first + i] = chunk[:, :, i * UNIT : (i + 1) * UNIT]
 
@@ -104,21 +112,40 @@ def tile_encoder_flows_pb_kernel(tc, flows, x_gcn1, W2, b2, out):
                 nc.tensor.transpose(turned[:, t, :], x_rows[g][:, a * PACK + t, :], identity[:])
             nc.scalar.copy(out=x_cols[g][:, a * PACK : (a + 1) * PACK, :], in_=turned[:])
 
-        def degree_unit(g, a, u):
+        def degree_sums(g, a, u, part, rows):
             for n in range(u * UNIT_TILES, (u + 1) * UNIT_TILES):
-                for t in range(PACK):
+                first = part * NODE_TILES + n
+                for t in rows:
                     nc.tensor.matmul(
-                        out=deg_parts[:, g, n, a : a + 1],
+                        out=deg_parts[g][:, first : first + COPIES[g]],
                         lhsT=raw[g, a, u][:, t, (n % UNIT_TILES) * P : (n % UNIT_TILES + 1) * P],
-                        rhs=ones[:, 0:1],
-                        start=(t == 0),
-                        stop=(t == PACK - 1),
+                        rhs=ones[:, 0 : COPIES[g]],
+                        start=(t == rows[0]),
+                        stop=(t == rows[-1]),
                     )
+
+        def degree_unit(g, a, u):
+            degree_sums(g, a, u, a, range(PACK))
+
+        def degree_half(g, a, u, half):
+            degree_sums(g, a, u, 2 * a - 1 + half, (2 * half, 2 * half + 1))
 
         def regroup(copy, g, a, u, first, last):
             copy(
                 out=grouped[g, a, u][:, first:last, :].rearrange("p (c i) t -> p c t i", i=RUN),
                 in_=raw[g, a, u][:, :, first:last].rearrange("p t (c i) -> p c t i", i=RUN),
+            )
+
+        def warm():
+            bank = acc_psum.tile([P, UNIT], F32, name="bank")
+            nc.tensor.matmul_mx(
+                out=bank[:],
+                lhsT=flow_codes[0][:, 0, 0:P].bitcast(FP8X4),
+                lhsT_scale=flow_scales[0][:, 0, 0:P],
+                rhs=flow_codes[0][:, 0, 0:UNIT].bitcast(FP8X4),
+                rhs_scale=flow_scales[0][:, 0, 0:UNIT],
+                start=True,
+                stop=True,
             )
 
         def open_unit(g, a, u):
@@ -144,7 +171,12 @@ def tile_encoder_flows_pb_kernel(tc, flows, x_gcn1, W2, b2, out):
 
         def degrees(g):
             deg[g] = small.tile([P, NODE_TILES], F32, name="deg")
-            nc.vector.tensor_reduce(out=deg[g][:], in_=deg_parts[:, g, :, :], axis=AXIS.X, op=ALU.add)
+            nc.vector.tensor_reduce(
+                out=deg[g][:],
+                in_=deg_parts[g][:, : DEG_PARTS[g] * NODE_TILES].rearrange("p (k n) -> p n k", n=NODE_TILES),
+                axis=AXIS.X,
+                op=ALU.add,
+            )
 
         def roots(g):
             safe = small.tile([P, NODE_TILES], F32, name="safe")
@@ -289,159 +321,247 @@ def tile_encoder_flows_pb_kernel(tc, flows, x_gcn1, W2, b2, out):
         load_rows(0, 1, 2, 2)
         nc.sync.dma_start(out=w2_sb[:], in_=W2)
         nc.sync.dma_start(out=bias_row[0:1, :], in_=b2.unsqueeze(0))
-        load_features(0)
-        arrivals = [(g, a, h) for g in range(GRAPHS) for a in range(PASSES) for h in range(UNITS // 2)]
-        for g, a, h in arrivals[4:10]:
-            load_rows(g, a, 2 * h, 2)
-            if (g, a, h) == (0, PASSES - 1, 1):
-                load_features(1)
-        late_loads = arrivals[10:]
-
+        load_rows(0, 2, 0, 2)
         waiting = []
 
         def quantise_waiting():
             if waiting:
                 quantise_unit(*waiting.pop(0))
-        for k in range(PASSES * UNITS):
-            a, u = divmod(k, UNITS)
-            share = ([272,272,272,272,272,272,272,272,272,272,272,272,272,272,272,272])[k]
-            degree_unit(0, a, u)
-            regroup_unit(0, a, u, share)
-            if k == 15:
-                degrees(0)
-            regroup_vector(0, a, u, share)
-            if len(waiting) >= 1:
-                quantise_waiting()
-            waiting.append((0, a, u))
-            if k >= 3 and u % 2 == 1 and late_loads:
-                g, aa, h = late_loads.pop(0)
-                load_rows(g, aa, 2 * h, 2)
-            if k == 6:
-                spread = work_psum.tile([P, CHANNELS], F32, tag="work")
-                nc.tensor.matmul(out=spread[:], lhsT=ones[:], rhs=bias_row[:], start=True, stop=True)
-                nc.vector.tensor_copy(out=bias[:], in_=spread[:])
-            if 8 <= k < 8 + PASSES:
-                transpose_features(0, k - 8)
-        features_times_weights(0, 0)
+        degree_unit(0, 0, 0)
+        regroup_unit(0, 0, 0, 256)
+        regroup_vector(0, 0, 0, 256)
+        quantise_waiting()
+        waiting.append((0, 0, 0))
+        degree_unit(0, 0, 1)
+        regroup_unit(0, 0, 1, 256)
+        regroup_vector(0, 0, 1, 256)
+        quantise_waiting()
+        waiting.append((0, 0, 1))
+        degree_unit(0, 0, 2)
+        regroup_unit(0, 0, 2, 256)
+        regroup_vector(0, 0, 2, 256)
+        quantise_waiting()
+        waiting.append((0, 0, 2))
+        degree_unit(0, 0, 3)
+        regroup_unit(0, 0, 3, 256)
+        regroup_vector(0, 0, 3, 256)
+        quantise_waiting()
+        waiting.append((0, 0, 3))
+        load_rows(0, 2, 2, 2)
+        degree_unit(0, 1, 0)
+        regroup_unit(0, 1, 0, 256)
+        regroup_vector(0, 1, 0, 256)
+        quantise_waiting()
+        waiting.append((0, 1, 0))
+        degree_unit(0, 1, 1)
+        regroup_unit(0, 1, 1, 256)
+        regroup_vector(0, 1, 1, 256)
+        quantise_waiting()
+        waiting.append((0, 1, 1))
+        load_rows(0, 3, 0, 2)
+        load_features(0)
+        degree_unit(0, 1, 2)
+        regroup_unit(0, 1, 2, 256)
+        regroup_vector(0, 1, 2, 256)
+        quantise_waiting()
+        waiting.append((0, 1, 2))
+        spread = work_psum.tile([P, CHANNELS], F32, tag="work")
+        nc.tensor.matmul(out=spread[:], lhsT=ones[:], rhs=bias_row[:], start=True, stop=True)
+        nc.vector.tensor_copy(out=bias[:], in_=spread[:])
+        degree_unit(0, 1, 3)
+        regroup_unit(0, 1, 3, 256)
+        regroup_vector(0, 1, 3, 256)
+        quantise_waiting()
+        waiting.append((0, 1, 3))
+        load_rows(0, 3, 2, 2)
+        degree_unit(0, 2, 0)
+        regroup_unit(0, 2, 0, 256)
+        regroup_vector(0, 2, 0, 256)
+        quantise_waiting()
+        waiting.append((0, 2, 0))
+        degree_unit(0, 2, 1)
+        regroup_unit(0, 2, 1, 256)
+        regroup_vector(0, 2, 1, 256)
+        quantise_waiting()
+        waiting.append((0, 2, 1))
+        load_rows(1, 0, 0, 2)
+        degree_unit(0, 2, 2)
+        regroup_unit(0, 2, 2, 256)
+        regroup_vector(0, 2, 2, 256)
+        quantise_waiting()
+        waiting.append((0, 2, 2))
+        degree_unit(0, 2, 3)
+        regroup_unit(0, 2, 3, 256)
+        regroup_vector(0, 2, 3, 256)
+        quantise_waiting()
+        waiting.append((0, 2, 3))
+        load_rows(1, 0, 2, 2)
+        load_rows(1, 1, 0, 4)
+        load_rows(1, 2, 0, 4)
+        load_rows(1, 3, 0, 4)
+        load_features(1)
+        degree_unit(0, 3, 0)
+        regroup_unit(0, 3, 0, 256)
+        regroup_vector(0, 3, 0, 256)
+        quantise_waiting()
+        waiting.append((0, 3, 0))
+        transpose_features(0, 0)
+        degree_unit(0, 3, 1)
+        regroup_unit(0, 3, 1, 256)
+        regroup_vector(0, 3, 1, 256)
+        quantise_waiting()
+        waiting.append((0, 3, 1))
+        transpose_features(0, 1)
+        degree_unit(0, 3, 2)
+        regroup_unit(0, 3, 2, 256)
+        regroup_vector(0, 3, 2, 256)
+        quantise_waiting()
+        waiting.append((0, 3, 2))
+        transpose_features(0, 2)
+        degree_unit(0, 3, 3)
+        regroup_unit(0, 3, 3, 256)
+        regroup_vector(0, 3, 3, 256)
+        degrees(0)
+        quantise_waiting()
+        waiting.append((0, 3, 3))
+        transpose_features(0, 3)
         roots(0)
+        regroup_unit(1, 0,0, 160)
+        regroup_vector(1, 0,0, 160)
+        quantise_waiting()
+        features_times_weights(0, 0)
+        inverses(0)
+        pick_inverses(0)
+        regroup_vector(1, 0,1, 160)
+        regroup_unit(1, 0,1, 160)
+        message_inverses(0)
+        scale_messages(0, 0)
+        features_times_weights(0, 1)
+        degree_unit(1, 0, 0)
+        scale_messages(0, 1)
+        features_times_weights(0, 2)
+        degree_unit(1, 0, 1)
+        scale_messages(0, 2)
+        features_times_weights(0, 3)
+        degree_unit(1, 0, 2)
+        scale_messages(0, 3)
+        quantise_messages(0, 0)
+        quantise_messages(0, 1)
+        degree_unit(1, 0, 3)
+        quantise_messages(0, 2)
+        quantise_messages(0, 3)
+        degree_half(1, 1, 0, 0)
+        degree_half(1, 1, 1, 0)
+        degree_half(1, 1, 2, 0)
+        degree_half(1, 1, 3, 0)
+        regroup_vector(1, 0,2, 64)
+        quantise_unit(1, 0,0)
+        regroup_unit(1, 0,2, 64)
+        multiply(0, 0)
+        degree_half(1, 1, 0, 1)
+        degree_half(1, 1, 1, 1)
+        degree_half(1, 1, 2, 1)
+        degree_half(1, 1, 3, 1)
+        quantise_unit(1, 0,1)
+        regroup_unit(1, 0,3, 64)
+        regroup_vector(1, 0,3, 64)
+        finish(0, 0)
+        multiply(0, 1)
+        degree_half(1, 2, 0, 0)
+        degree_half(1, 2, 1, 0)
+        degree_half(1, 2, 2, 0)
+        degree_half(1, 2, 3, 0)
+        regroup_vector(1, 1,0, 64)
+        quantise_unit(1, 0,2)
+        regroup_unit(1, 1,0, 64)
+        finish(0, 1)
+        multiply(0, 2)
+        degree_half(1, 2, 0, 1)
+        degree_half(1, 2, 1, 1)
+        degree_half(1, 2, 2, 1)
+        degree_half(1, 2, 3, 1)
+        regroup_vector(1, 1,1, 64)
+        quantise_unit(1, 0,3)
+        regroup_unit(1, 1,1, 64)
+        degree_half(1, 3, 0, 0)
+        degree_half(1, 3, 1, 0)
+        degree_half(1, 3, 2, 0)
+        degree_half(1, 3, 3, 0)
+        regroup_vector(1, 1,2, 64)
+        quantise_unit(1, 1,0)
+        regroup_unit(1, 1,2, 64)
+        finish(0, 2)
+        degree_half(1, 3, 0, 1)
+        degree_half(1, 3, 1, 1)
+        degree_half(1, 3, 2, 1)
+        degree_half(1, 3, 3, 1)
+        regroup_vector(1, 1,3, 64)
+        quantise_unit(1, 1,1)
+        regroup_unit(1, 1,3, 64)
+        regroup_vector(1, 2,0, 96)
+        regroup_unit(1, 2,0, 96)
+        degrees(1)
+        roots(1)
+        multiply(0, 3)
         transpose_features(1, 0)
         transpose_features(1, 1)
         transpose_features(1, 2)
         transpose_features(1, 3)
-        inverses(0)
-        pick_inverses(0)
-        degree_unit(1, 0, 0)
-        regroup_unit(1, 0,0, 192)
-        regroup_vector(1, 0,0, 192)
-        quantise_waiting()
-        degree_unit(1, 0, 1)
-        features_times_weights(0, 0)
-        regroup_vector(1, 0,1, 192)
-        regroup_unit(1, 0,1, 192)
-        degree_unit(1, 0, 2)
-        message_inverses(0)
-        scale_messages(0, 0)
-        features_times_weights(0, 1)
-        degree_unit(1, 0, 3)
-        scale_messages(0, 1)
-        features_times_weights(0, 2)
-        degree_unit(1, 1, 0)
-        regroup_unit(1, 0,2, 0)
-        scale_messages(0, 2)
-        features_times_weights(0, 3)
-        degree_unit(1, 1, 1)
-        scale_messages(0, 3)
-        quantise_messages(0, 0)
-        quantise_messages(0, 1)
-        degree_unit(1, 1, 2)
-        degree_unit(1, 1, 3)
-        quantise_messages(0, 2)
-        quantise_messages(0, 3)
-        degree_unit(1, 2, 0)
-        degree_unit(1, 2, 1)
-        multiply(0, 0)
-        quantise_unit(1, 0,0)
-        quantise_unit(1, 0,1)
-        regroup_unit(1, 0,3, 0)
-        degree_unit(1, 2, 2)
-        degree_unit(1, 2, 3)
-        multiply(0, 1)
-        quantise_unit(1, 0,2)
-        regroup_unit(1, 1,0, 96)
-        finish(0, 0)
-        regroup_vector(1, 1,0, 96)
-        regroup_vector(1, 1,1, 96)
-        degree_unit(1, 3, 0)
-        degree_unit(1, 3, 1)
-        quantise_unit(1, 0,3)
-        regroup_unit(1, 1,1, 96)
-        finish(0, 1)
-        features_times_weights(1, 0)
-        degree_unit(1, 3, 2)
-        degree_unit(1, 3, 3)
-        multiply(0, 2)
-        regroup_vector(1, 1,2, 96)
-        regroup_vector(1, 1,3, 96)
-        quantise_unit(1, 1,0)
-        regroup_unit(1, 1,2, 96)
-        finish(0, 2)
-        degrees(1)
-        roots(1)
-        multiply(0, 3)
-        quantise_unit(1, 1,1)
-        regroup_unit(1, 1,3, 96)
+        quantise_unit(1, 1,2)
+        regroup_vector(1, 3,0, 96)
         inverses(1)
         pick_inverses(1)
-        finish(0, 3)
+        features_times_weights(1, 0)
         multiply(0, 4)
-        quantise_unit(1, 1,2)
-        regroup_unit(1, 2,0, 0)
-        finish(0, 4)
+        finish(0, 3)
+        regroup_vector(1, 2,1, 64)
         message_inverses(1)
         scale_messages(1, 0)
         features_times_weights(1, 1)
-        multiply(0, 5)
         scale_messages(1, 1)
         features_times_weights(1, 2)
         scale_messages(1, 2)
         features_times_weights(1, 3)
-        multiply(0, 6)
+        finish(0, 4)
+        multiply(0, 5)
         scale_messages(1, 3)
         quantise_messages(1, 0)
         quantise_messages(1, 1)
         quantise_messages(1, 2)
         quantise_messages(1, 3)
+        multiply(0, 6)
         quantise_unit(1, 1,3)
-        regroup_unit(1, 3,0, 0)
+        regroup_unit(1, 3,0, 96)
+        finish(0, 5)
+        multiply(0, 7)
         quantise_unit(1, 2,0)
-        regroup_unit(1, 2,1, 0)
+        regroup_unit(1, 2,1, 64)
+        regroup_vector(1, 3,1, 0)
+        finish(0, 6)
         quantise_unit(1, 3,0)
         regroup_unit(1, 3,1, 0)
-        multiply(0, 7)
-        quantise_unit(1, 2,1)
-        regroup_unit(1, 2,2, 48)
-        finish(0, 5)
+        finish(0, 7)
         multiply(1, 0)
         multiply(1, 1)
+        quantise_unit(1, 2,1)
+        regroup_unit(1, 2,2, 0)
+        finish(1, 0)
         quantise_unit(1, 3,1)
-        regroup_unit(1, 3,2, 48)
-        finish(0, 6)
-        finish(0, 7)
+        regroup_unit(1, 3,2, 0)
+        finish(1, 1)
         multiply(1, 2)
         multiply(1, 3)
-        regroup_vector(1, 2,2, 48)
+        regroup_vector(1, 2,2, 0)
         quantise_unit(1, 2,2)
-        regroup_unit(1, 2,3, 48)
-        finish(1, 0)
-        finish(1, 1)
-        regroup_vector(1, 3,2, 48)
-        quantise_unit(1, 3,2)
-        regroup_unit(1, 3,3, 48)
-        multiply(1, 4)
+        regroup_unit(1, 2,3, 0)
         finish(1, 2)
-        multiply(1, 5)
+        regroup_vector(1, 3,2, 0)
+        quantise_unit(1, 3,2)
+        regroup_unit(1, 3,3, 0)
         finish(1, 3)
-        regroup_vector(1, 2,3, 48)
+        multiply(1, 4)
+        multiply(1, 5)
+        regroup_vector(1, 2,3, 0)
         quantise_unit(1, 2,3)
         begin_last(12)
         begin_last(13)
@@ -449,7 +569,7 @@ def tile_encoder_flows_pb_kernel(tc, flows, x_gcn1, W2, b2, out):
         begin_last(15)
         finish(1, 4)
         finish(1, 5)
-        regroup_vector(1, 3,3, 48)
+        regroup_vector(1, 3,3, 0)
         quantise_unit(1, 3,3)
         end_last(12)
         end_last(13)

@@ -44,7 +44,7 @@ def tile_encoder_flows_pb_kernel(tc, flows, x_gcn1, W2, b2, out):
         raw_pool = ctx.enter_context(tc.tile_pool(name="raw", bufs=9))
         grouped_pool = ctx.enter_context(tc.tile_pool(name="grouped", bufs=6))
         small = ctx.enter_context(tc.tile_pool(name="small", bufs=2))
-        result_pool = ctx.enter_context(tc.tile_pool(name="result", bufs=3))
+        result_pool = ctx.enter_context(tc.tile_pool(name="result", bufs=4))
         deg_psum = ctx.enter_context(tc.psum_pool(name="deg_psum", bufs=1))
         work_psum = ctx.enter_context(tc.psum_pool(name="work_psum", bufs=4))
         acc_psum = ctx.enter_context(tc.psum_pool(name="acc_psum", bufs=3))
@@ -264,7 +264,10 @@ def tile_encoder_flows_pb_kernel(tc, flows, x_gcn1, W2, b2, out):
                 )
 
         def multiply(g, j):
-            bank = acc_psum.tile([P, PAIR, CHANNELS], F32, name="bank")
+            if g == 1 and j < 4:
+                bank = work_psum.tile([P, PAIR, CHANNELS], F32, name="bank", tag="work")
+            else:
+                bank = acc_psum.tile([P, PAIR, CHANNELS], F32, name="bank")
             for i in range(PAIR):
                 acc[g, PAIR * j + i] = bank[:, i, :]
                 product_passes(g, PAIR * j + i, range(PASSES))
@@ -359,7 +362,6 @@ def tile_encoder_flows_pb_kernel(tc, flows, x_gcn1, W2, b2, out):
         quantise_waiting()
         waiting.append((0, 1, 1))
         load_rows(0, 3, 0, 2)
-        load_features(0)
         degree_unit(0, 1, 2)
         regroup_unit(0, 1, 2, 256)
         regroup_vector(0, 1, 2, 256)
@@ -374,6 +376,7 @@ def tile_encoder_flows_pb_kernel(tc, flows, x_gcn1, W2, b2, out):
         quantise_waiting()
         waiting.append((0, 1, 3))
         load_rows(0, 3, 2, 2)
+        load_features(0)
         degree_unit(0, 2, 0)
         regroup_unit(0, 2, 0, 256)
         regroup_vector(0, 2, 0, 256)
@@ -405,172 +408,168 @@ def tile_encoder_flows_pb_kernel(tc, flows, x_gcn1, W2, b2, out):
         regroup_vector(0, 3, 0, 256)
         quantise_waiting()
         waiting.append((0, 3, 0))
-        transpose_features(0, 0)
         degree_unit(0, 3, 1)
         regroup_unit(0, 3, 1, 256)
         regroup_vector(0, 3, 1, 256)
         quantise_waiting()
         waiting.append((0, 3, 1))
-        transpose_features(0, 1)
         degree_unit(0, 3, 2)
         regroup_unit(0, 3, 2, 256)
         regroup_vector(0, 3, 2, 256)
         quantise_waiting()
         waiting.append((0, 3, 2))
-        transpose_features(0, 2)
         degree_unit(0, 3, 3)
         regroup_unit(0, 3, 3, 256)
         regroup_vector(0, 3, 3, 256)
         degrees(0)
+        roots(0)
         quantise_waiting()
         waiting.append((0, 3, 3))
-        transpose_features(0, 3)
-        roots(0)
+        transpose_features(0, 0)
+        transpose_features(0, 1)
         regroup_unit(1, 0,0, 160)
         regroup_vector(1, 0,0, 160)
         quantise_waiting()
+        warm()
         features_times_weights(0, 0)
         inverses(0)
         pick_inverses(0)
+        transpose_features(0, 2)
+        transpose_features(0, 3)
+        warm()
+        degree_unit(1, 0, 0)
+        degree_unit(1, 0, 1)
         regroup_vector(1, 0,1, 160)
         regroup_unit(1, 0,1, 160)
         message_inverses(0)
         scale_messages(0, 0)
         features_times_weights(0, 1)
-        degree_unit(1, 0, 0)
+        degree_unit(1, 0, 2)
         scale_messages(0, 1)
         features_times_weights(0, 2)
-        degree_unit(1, 0, 1)
+        degree_unit(1, 0, 3)
         scale_messages(0, 2)
         features_times_weights(0, 3)
-        degree_unit(1, 0, 2)
         scale_messages(0, 3)
-        quantise_messages(0, 0)
-        quantise_messages(0, 1)
-        degree_unit(1, 0, 3)
-        quantise_messages(0, 2)
-        quantise_messages(0, 3)
         degree_half(1, 1, 0, 0)
         degree_half(1, 1, 1, 0)
         degree_half(1, 1, 2, 0)
         degree_half(1, 1, 3, 0)
-        regroup_vector(1, 0,2, 64)
+        quantise_messages(0, 0)
+        quantise_messages(0, 1)
+        quantise_messages(0, 2)
+        quantise_messages(0, 3)
+        regroup_vector(1, 0,2, 128)
         quantise_unit(1, 0,0)
-        regroup_unit(1, 0,2, 64)
+        regroup_unit(1, 0,2, 128)
         multiply(0, 0)
         degree_half(1, 1, 0, 1)
         degree_half(1, 1, 1, 1)
         degree_half(1, 1, 2, 1)
         degree_half(1, 1, 3, 1)
         quantise_unit(1, 0,1)
-        regroup_unit(1, 0,3, 64)
-        regroup_vector(1, 0,3, 64)
+        regroup_unit(1, 0,3, 128)
+        regroup_vector(1, 0,3, 128)
         finish(0, 0)
         multiply(0, 1)
         degree_half(1, 2, 0, 0)
         degree_half(1, 2, 1, 0)
         degree_half(1, 2, 2, 0)
         degree_half(1, 2, 3, 0)
-        regroup_vector(1, 1,0, 64)
+        regroup_vector(1, 1,0, 128)
         quantise_unit(1, 0,2)
-        regroup_unit(1, 1,0, 64)
+        regroup_unit(1, 1,0, 128)
+        regroup_vector(1, 1,1, 128)
+        quantise_unit(1, 0,3)
+        regroup_unit(1, 1,1, 128)
         finish(0, 1)
-        multiply(0, 2)
         degree_half(1, 2, 0, 1)
         degree_half(1, 2, 1, 1)
         degree_half(1, 2, 2, 1)
         degree_half(1, 2, 3, 1)
-        regroup_vector(1, 1,1, 64)
-        quantise_unit(1, 0,3)
-        regroup_unit(1, 1,1, 64)
+        multiply(0, 2)
+        regroup_vector(1, 1,2, 96)
+        quantise_unit(1, 1,0)
+        regroup_unit(1, 1,2, 96)
         degree_half(1, 3, 0, 0)
         degree_half(1, 3, 1, 0)
         degree_half(1, 3, 2, 0)
         degree_half(1, 3, 3, 0)
-        regroup_vector(1, 1,2, 64)
-        quantise_unit(1, 1,0)
-        regroup_unit(1, 1,2, 64)
-        finish(0, 2)
+        regroup_vector(1, 1,3, 96)
+        quantise_unit(1, 1,1)
+        regroup_unit(1, 1,3, 96)
         degree_half(1, 3, 0, 1)
         degree_half(1, 3, 1, 1)
         degree_half(1, 3, 2, 1)
         degree_half(1, 3, 3, 1)
-        regroup_vector(1, 1,3, 64)
-        quantise_unit(1, 1,1)
-        regroup_unit(1, 1,3, 64)
-        regroup_vector(1, 2,0, 96)
-        regroup_unit(1, 2,0, 96)
+        finish(0, 2)
+        quantise_unit(1, 1,2)
+        regroup_unit(1, 2,0, 0)
         degrees(1)
         roots(1)
-        multiply(0, 3)
         transpose_features(1, 0)
         transpose_features(1, 1)
         transpose_features(1, 2)
         transpose_features(1, 3)
-        quantise_unit(1, 1,2)
-        regroup_vector(1, 3,0, 96)
+        warm()
+        warm()
         inverses(1)
         pick_inverses(1)
+        quantise_unit(1, 1,3)
+        regroup_unit(1, 3,0, 0)
         features_times_weights(1, 0)
-        multiply(0, 4)
-        finish(0, 3)
-        regroup_vector(1, 2,1, 64)
+        features_times_weights(1, 1)
+        multiply(0, 3)
         message_inverses(1)
         scale_messages(1, 0)
-        features_times_weights(1, 1)
-        scale_messages(1, 1)
         features_times_weights(1, 2)
-        scale_messages(1, 2)
+        multiply(0, 4)
+        scale_messages(1, 1)
         features_times_weights(1, 3)
-        finish(0, 4)
+        scale_messages(1, 2)
+        finish(0, 3)
         multiply(0, 5)
         scale_messages(1, 3)
+        finish(0, 4)
         quantise_messages(1, 0)
         quantise_messages(1, 1)
         quantise_messages(1, 2)
         quantise_messages(1, 3)
         multiply(0, 6)
-        quantise_unit(1, 1,3)
-        regroup_unit(1, 3,0, 96)
-        finish(0, 5)
-        multiply(0, 7)
         quantise_unit(1, 2,0)
-        regroup_unit(1, 2,1, 64)
-        regroup_vector(1, 3,1, 0)
-        finish(0, 6)
+        regroup_unit(1, 2,1, 0)
         quantise_unit(1, 3,0)
         regroup_unit(1, 3,1, 0)
-        finish(0, 7)
+        multiply(0, 7)
         multiply(1, 0)
+        finish(0, 5)
         multiply(1, 1)
+        finish(0, 6)
+        finish(0, 7)
         quantise_unit(1, 2,1)
         regroup_unit(1, 2,2, 0)
-        finish(1, 0)
         quantise_unit(1, 3,1)
         regroup_unit(1, 3,2, 0)
-        finish(1, 1)
+        finish(1, 0)
         multiply(1, 2)
         multiply(1, 3)
-        regroup_vector(1, 2,2, 0)
+        finish(1, 1)
         quantise_unit(1, 2,2)
         regroup_unit(1, 2,3, 0)
         finish(1, 2)
-        regroup_vector(1, 3,2, 0)
         quantise_unit(1, 3,2)
         regroup_unit(1, 3,3, 0)
         finish(1, 3)
         multiply(1, 4)
         multiply(1, 5)
-        regroup_vector(1, 2,3, 0)
         quantise_unit(1, 2,3)
         begin_last(12)
         begin_last(13)
         begin_last(14)
         begin_last(15)
         finish(1, 4)
-        finish(1, 5)
-        regroup_vector(1, 3,3, 0)
         quantise_unit(1, 3,3)
+        finish(1, 5)
         end_last(12)
         end_last(13)
         finish(1, 6)

@@ -48,7 +48,6 @@ def tile_encoder_flows_pb_kernel(tc, flows, x_gcn1, W2, b2, out):
         deg_psum = ctx.enter_context(tc.psum_pool(name="deg_psum", bufs=1))
         work_psum = ctx.enter_context(tc.psum_pool(name="work_psum", bufs=4))
         acc_psum = ctx.enter_context(tc.psum_pool(name="acc_psum", bufs=3))
-        ctx.enter_context(tc.manual_schedule())
 
         flow_codes = [
             keep.tile([P, PASSES, NODES], U32, name="flow_codes%d" % g, align_bytes=64)

@@ -135,18 +135,6 @@ def tile_encoder_flows_pb_kernel(tc, flows, x_gcn1, W2, b2, out):
                 in_=raw[g, a, u][:, :, first:last].rearrange("p t (c i) -> p c t i", i=RUN),
             )
 
-        def warm():
-            bank = acc_psum.tile([P, UNIT], F32, name="bank")
-            nc.tensor.matmul_mx(
-                out=bank[:],
-                lhsT=flow_codes[0][:, 0, 0:P].bitcast(FP8X4),
-                lhsT_scale=flow_scales[0][:, 0, 0:P],
-                rhs=flow_codes[0][:, 0, 0:UNIT].bitcast(FP8X4),
-                rhs_scale=flow_scales[0][:, 0, 0:UNIT],
-                start=True,
-                stop=True,
-            )
-
         def open_unit(g, a, u):
             if (g, a, u) not in grouped:
                 grouped[g, a, u] = grouped_pool.tile([P, UNIT, PACK], BF16, name="grouped", align_bytes=64)
@@ -296,9 +284,27 @@ def tile_encoder_flows_pb_kernel(tc, flows, x_gcn1, W2, b2, out):
                 in_=result[:],
             )
 
+        def normalise(g):
+            degrees(g)
+            roots(g)
+            inverses(g)
+            pick_inverses(g)
+            message_inverses(g)
+
+        def messages(g, beside):
+            for a in range(PASSES):
+                features_times_weights(g, a)
+                beside(a)
+                scale_messages(g, a)
+            for a in range(PASSES):
+                quantise_messages(g, a)
+
         load_rows(0, 0, 0, 1)
         load_rows(0, 0, 1, 1)
-        load_rows(0, 0, 2, 2)
+        halves = [(g, a, first) for g in range(GRAPHS) for a in range(PASSES) for first in (0, UNITS // 2)]
+        halves = halves[1 : 2 * PASSES + 2]
+        for g, a, first in halves[:3]:
+            load_rows(g, a, first, 2)
         ones = const.tile([P, P], BF16)
         nc.vector.memset(ones[:], 1.0)
         scratch = const.tile([P, 1], F32)
@@ -319,259 +325,84 @@ def tile_encoder_flows_pb_kernel(tc, flows, x_gcn1, W2, b2, out):
         nc.vector.tensor_reduce(
             out=residue[:], in_=identity_f32[:].rearrange("p (j t) -> p t j", t=PACK), axis=AXIS.X, op=ALU.add
         )
-        load_rows(0, 1, 0, 2)
-        load_rows(0, 1, 2, 2)
         nc.sync.dma_start(out=w2_sb[:], in_=W2)
         nc.sync.dma_start(out=bias_row[0:1, :], in_=b2.unsqueeze(0))
-        load_rows(0, 2, 0, 2)
-        waiting = []
+        load_rows(*halves[3], 2)
+        halves = halves[4:]
 
-        def quantise_waiting():
-            if waiting:
-                quantise_unit(*waiting.pop(0))
-        degree_unit(0, 0, 0)
-        regroup_unit(0, 0, 0, 256)
-        regroup_vector(0, 0, 0, 256)
-        quantise_waiting()
-        waiting.append((0, 0, 0))
-        degree_unit(0, 0, 1)
-        regroup_unit(0, 0, 1, 256)
-        regroup_vector(0, 0, 1, 256)
-        quantise_waiting()
-        waiting.append((0, 0, 1))
-        degree_unit(0, 0, 2)
-        regroup_unit(0, 0, 2, 256)
-        regroup_vector(0, 0, 2, 256)
-        quantise_waiting()
-        waiting.append((0, 0, 2))
-        degree_unit(0, 0, 3)
-        regroup_unit(0, 0, 3, 256)
-        regroup_vector(0, 0, 3, 256)
-        quantise_waiting()
-        waiting.append((0, 0, 3))
-        load_rows(0, 2, 2, 2)
-        degree_unit(0, 1, 0)
-        regroup_unit(0, 1, 0, 256)
-        regroup_vector(0, 1, 0, 256)
-        quantise_waiting()
-        waiting.append((0, 1, 0))
-        degree_unit(0, 1, 1)
-        regroup_unit(0, 1, 1, 256)
-        regroup_vector(0, 1, 1, 256)
-        quantise_waiting()
-        waiting.append((0, 1, 1))
-        load_rows(0, 3, 0, 2)
-        degree_unit(0, 1, 2)
-        regroup_unit(0, 1, 2, 256)
-        regroup_vector(0, 1, 2, 256)
-        quantise_waiting()
-        waiting.append((0, 1, 2))
-        spread = work_psum.tile([P, CHANNELS], F32, tag="work")
-        nc.tensor.matmul(out=spread[:], lhsT=ones[:], rhs=bias_row[:], start=True, stop=True)
-        nc.vector.tensor_copy(out=bias[:], in_=spread[:])
-        degree_unit(0, 1, 3)
-        regroup_unit(0, 1, 3, 256)
-        regroup_vector(0, 1, 3, 256)
-        quantise_waiting()
-        waiting.append((0, 1, 3))
-        load_rows(0, 3, 2, 2)
-        load_features(0)
-        degree_unit(0, 2, 0)
-        regroup_unit(0, 2, 0, 256)
-        regroup_vector(0, 2, 0, 256)
-        quantise_waiting()
-        waiting.append((0, 2, 0))
-        degree_unit(0, 2, 1)
-        regroup_unit(0, 2, 1, 256)
-        regroup_vector(0, 2, 1, 256)
-        quantise_waiting()
-        waiting.append((0, 2, 1))
-        load_rows(1, 0, 0, 2)
-        degree_unit(0, 2, 2)
-        regroup_unit(0, 2, 2, 256)
-        regroup_vector(0, 2, 2, 256)
-        quantise_waiting()
-        waiting.append((0, 2, 2))
-        degree_unit(0, 2, 3)
-        regroup_unit(0, 2, 3, 256)
-        regroup_vector(0, 2, 3, 256)
-        quantise_waiting()
-        waiting.append((0, 2, 3))
-        load_rows(1, 0, 2, 2)
-        load_rows(1, 1, 0, 4)
-        load_rows(1, 2, 0, 4)
-        load_rows(1, 3, 0, 4)
+        flows_of_0 = [(0, a, u) for a in range(PASSES) for u in range(UNITS)]
+        for k, unit in enumerate(flows_of_0):
+            degree_unit(*unit)
+            regroup_unit(*unit, 256)
+            regroup_vector(*unit, 256)
+            if k > 0:
+                quantise_unit(*flows_of_0[k - 1])
+            if k >= 3 and k % 2 == 1 and halves:
+                load_rows(*halves.pop(0), 2)
+                if len(halves) == 2:
+                    load_features(0)
+            if k == 6:
+                spread = work_psum.tile([P, CHANNELS], F32, tag="work")
+                nc.tensor.matmul(out=spread[:], lhsT=ones[:], rhs=bias_row[:], start=True, stop=True)
+                nc.vector.tensor_copy(out=bias[:], in_=spread[:])
+        for a in range(1, PASSES):
+            load_rows(1, a, 0, UNITS)
         load_features(1)
-        degree_unit(0, 3, 0)
-        regroup_unit(0, 3, 0, 256)
-        regroup_vector(0, 3, 0, 256)
-        quantise_waiting()
-        waiting.append((0, 3, 0))
-        degree_unit(0, 3, 1)
-        regroup_unit(0, 3, 1, 256)
-        regroup_vector(0, 3, 1, 256)
-        quantise_waiting()
-        waiting.append((0, 3, 1))
-        degree_unit(0, 3, 2)
-        regroup_unit(0, 3, 2, 256)
-        regroup_vector(0, 3, 2, 256)
-        quantise_waiting()
-        waiting.append((0, 3, 2))
-        degree_unit(0, 3, 3)
-        regroup_unit(0, 3, 3, 256)
-        regroup_vector(0, 3, 3, 256)
-        degrees(0)
-        roots(0)
-        quantise_waiting()
-        waiting.append((0, 3, 3))
-        transpose_features(0, 0)
-        transpose_features(0, 1)
-        regroup_unit(1, 0,0, 160)
-        regroup_vector(1, 0,0, 160)
-        quantise_waiting()
-        warm()
-        features_times_weights(0, 0)
-        inverses(0)
-        pick_inverses(0)
-        transpose_features(0, 2)
-        transpose_features(0, 3)
-        warm()
-        degree_unit(1, 0, 0)
-        degree_unit(1, 0, 1)
-        regroup_vector(1, 0,1, 160)
-        regroup_unit(1, 0,1, 160)
-        message_inverses(0)
-        scale_messages(0, 0)
-        features_times_weights(0, 1)
-        degree_unit(1, 0, 2)
-        scale_messages(0, 1)
-        features_times_weights(0, 2)
-        degree_unit(1, 0, 3)
-        scale_messages(0, 2)
-        features_times_weights(0, 3)
-        scale_messages(0, 3)
-        degree_half(1, 1, 0, 0)
-        degree_half(1, 1, 1, 0)
-        degree_half(1, 1, 2, 0)
-        degree_half(1, 1, 3, 0)
-        quantise_messages(0, 0)
-        quantise_messages(0, 1)
-        quantise_messages(0, 2)
-        quantise_messages(0, 3)
-        regroup_vector(1, 0,2, 128)
-        quantise_unit(1, 0,0)
-        regroup_unit(1, 0,2, 128)
-        multiply(0, 0)
-        degree_half(1, 1, 0, 1)
-        degree_half(1, 1, 1, 1)
-        degree_half(1, 1, 2, 1)
-        degree_half(1, 1, 3, 1)
-        quantise_unit(1, 0,1)
-        regroup_unit(1, 0,3, 128)
-        regroup_vector(1, 0,3, 128)
-        finish(0, 0)
-        multiply(0, 1)
-        degree_half(1, 2, 0, 0)
-        degree_half(1, 2, 1, 0)
-        degree_half(1, 2, 2, 0)
-        degree_half(1, 2, 3, 0)
-        regroup_vector(1, 1,0, 128)
-        quantise_unit(1, 0,2)
-        regroup_unit(1, 1,0, 128)
-        regroup_vector(1, 1,1, 128)
-        quantise_unit(1, 0,3)
-        regroup_unit(1, 1,1, 128)
-        finish(0, 1)
-        degree_half(1, 2, 0, 1)
-        degree_half(1, 2, 1, 1)
-        degree_half(1, 2, 2, 1)
-        degree_half(1, 2, 3, 1)
-        multiply(0, 2)
-        regroup_vector(1, 1,2, 96)
-        quantise_unit(1, 1,0)
-        regroup_unit(1, 1,2, 96)
-        degree_half(1, 3, 0, 0)
-        degree_half(1, 3, 1, 0)
-        degree_half(1, 3, 2, 0)
-        degree_half(1, 3, 3, 0)
-        regroup_vector(1, 1,3, 96)
-        quantise_unit(1, 1,1)
-        regroup_unit(1, 1,3, 96)
-        degree_half(1, 3, 0, 1)
-        degree_half(1, 3, 1, 1)
-        degree_half(1, 3, 2, 1)
-        degree_half(1, 3, 3, 1)
-        finish(0, 2)
-        quantise_unit(1, 1,2)
-        regroup_unit(1, 2,0, 0)
-        degrees(1)
-        roots(1)
-        transpose_features(1, 0)
-        transpose_features(1, 1)
-        transpose_features(1, 2)
-        transpose_features(1, 3)
-        warm()
-        warm()
-        inverses(1)
-        pick_inverses(1)
-        quantise_unit(1, 1,3)
-        regroup_unit(1, 3,0, 0)
-        features_times_weights(1, 0)
-        features_times_weights(1, 1)
-        multiply(0, 3)
-        message_inverses(1)
-        scale_messages(1, 0)
-        features_times_weights(1, 2)
-        multiply(0, 4)
-        scale_messages(1, 1)
-        features_times_weights(1, 3)
-        scale_messages(1, 2)
-        finish(0, 3)
-        multiply(0, 5)
-        scale_messages(1, 3)
-        finish(0, 4)
-        quantise_messages(1, 0)
-        quantise_messages(1, 1)
-        quantise_messages(1, 2)
-        quantise_messages(1, 3)
-        multiply(0, 6)
-        quantise_unit(1, 2,0)
-        regroup_unit(1, 2,1, 0)
-        quantise_unit(1, 3,0)
-        regroup_unit(1, 3,1, 0)
-        multiply(0, 7)
-        multiply(1, 0)
-        finish(0, 5)
-        multiply(1, 1)
-        finish(0, 6)
-        finish(0, 7)
-        quantise_unit(1, 2,1)
-        regroup_unit(1, 2,2, 0)
-        quantise_unit(1, 3,1)
-        regroup_unit(1, 3,2, 0)
-        finish(1, 0)
-        multiply(1, 2)
-        multiply(1, 3)
-        finish(1, 1)
-        quantise_unit(1, 2,2)
-        regroup_unit(1, 2,3, 0)
-        finish(1, 2)
-        quantise_unit(1, 3,2)
-        regroup_unit(1, 3,3, 0)
-        finish(1, 3)
-        multiply(1, 4)
-        multiply(1, 5)
-        quantise_unit(1, 2,3)
-        begin_last(12)
-        begin_last(13)
-        begin_last(14)
-        begin_last(15)
-        finish(1, 4)
-        quantise_unit(1, 3,3)
-        finish(1, 5)
-        end_last(12)
-        end_last(13)
+
+        ctx.enter_context(tc.manual_schedule(engines={mybir.EngineType.PE}))
+
+        for a in range(PASSES):
+            transpose_features(0, a)
+        normalise(0)
+        messages(0, lambda a: degree_unit(1, 0, a))
+        quantise_unit(*flows_of_0[-1])
+
+        flows_of_1 = [(1, a, u) for a in range(2) for u in range(UNITS)]
+        flows_of_1 += [(1, a, u) for u in range(UNITS) for a in range(2, PASSES)]
+
+        def step(k):
+            share = 160 if k < 2 else 128 if k < 6 else 96 if k < 8 else 0
+            regroup_unit(*flows_of_1[k], share)
+            regroup_vector(*flows_of_1[k], share)
+            if k > 0:
+                quantise_unit(*flows_of_1[k - 1])
+
+        for k in range(6):
+            step(k)
+            for u in range(UNITS):
+                degree_half(1, 1 + k // 2, u, k % 2)
+            if k % 2 == 0:
+                multiply(0, k // 2)
+            else:
+                finish(0, k // 2)
+
+        def next_product(a):
+            multiply(0, 3 + a)
+            if a > 0:
+                finish(0, 2 + a)
+
+        for a in range(PASSES):
+            transpose_features(1, a)
+        with tc.high_priority():
+            normalise(1)
+        messages(1, next_product)
+        for k in range(6, 16):
+            step(k)
+            if k == 6:
+                multiply(0, 7)
+                finish(0, 6)
+            if k == 7:
+                finish(0, 7)
+            if k >= 10 and k % 2 == 0:
+                multiply(1, k - 10)
+                multiply(1, k - 9)
+            if k >= 11 and k % 2 == 1:
+                finish(1, k - 11)
+                finish(1, k - 10)
+        for n in range(12, 16):
+            begin_last(n)
+        quantise_unit(*flows_of_1[-1])
+        for n in range(12, 16):
+            end_last(n)
         finish(1, 6)
-        end_last(14)
-        end_last(15)
         finish(1, 7)

from contextlib import ExitStack

import concourse.mybir as mybir
from concourse.masks import make_identity

F32 = mybir.dt.float32
BF16 = mybir.dt.bfloat16
U32 = mybir.dt.uint32
U8 = mybir.dt.uint8
FP8X4 = mybir.dt.float8_e4m3fn_x4
ALU = mybir.AluOpType
AXIS = mybir.AxisListType

P = 128
PACK = 4
QUAD = 32
QUADS = P // QUAD
GRAPHS = 2
NODES = 2048
FEATURES = 128
CHANNELS = 256
PASSES = NODES // (P * PACK)
NODE_TILES = NODES // P
UNIT = 512
UNITS = NODES // UNIT
UNIT_TILES = UNIT // P
RUN = 4
HALF = CHANNELS // 2
PAIR = 2
PAIRS = NODE_TILES // PAIR
DEG_PARTS = (PASSES, 2 * PASSES - 1)
COPIES = (2, 24)
DEG_COLUMNS = [DEG_PARTS[g] * NODE_TILES + COPIES[g] for g in range(GRAPHS)]
RAW_BUFS = {1: 2, 2: 4, 4: 3}

FLOPS = 2 * GRAPHS * NODES * NODES * CHANNELS + 2 * GRAPHS * NODES * FEATURES * CHANNELS


def tile_encoder_flows_pb_kernel(tc, flows, x_gcn1, W2, b2, out):
    nc = tc.nc
    with ExitStack() as ctx:
        const = ctx.enter_context(tc.tile_pool(name="const", bufs=1))
        keep = ctx.enter_context(tc.tile_pool(name="keep", bufs=1))
        raw_pool = ctx.enter_context(tc.tile_pool(name="raw", bufs=9))
        grouped_pool = ctx.enter_context(tc.tile_pool(name="grouped", bufs=6))
        small = ctx.enter_context(tc.tile_pool(name="small", bufs=2))
        result_pool = ctx.enter_context(tc.tile_pool(name="result", bufs=4))
        deg_psum = ctx.enter_context(tc.psum_pool(name="deg_psum", bufs=1))
        work_psum = ctx.enter_context(tc.psum_pool(name="work_psum", bufs=4))
        acc_psum = ctx.enter_context(tc.psum_pool(name="acc_psum", bufs=3))

        flow_codes = [
            keep.tile([P, PASSES, NODES], U32, name="flow_codes%d" % g, align_bytes=64)
            for g in range(GRAPHS)
        ]
        flow_scales = [
            keep.tile([P, PASSES, NODES], U8, name="flow_scales%d" % g, align_bytes=64)
            for g in range(GRAPHS)
        ]
        msg_codes = [
            keep.tile([P, PASSES, CHANNELS], U32, name="msg_codes%d" % g, align_bytes=64)
            for g in range(GRAPHS)
        ]
        msg_scales = [
            keep.tile([P, PASSES, CHANNELS], U8, name="msg_scales%d" % g, align_bytes=64)
            for g in range(GRAPHS)
        ]
        w2_sb = const.tile([FEATURES, CHANNELS], BF16)
        bias_row = const.tile([P, CHANNELS], BF16)
        bias = const.tile([P, CHANNELS], F32)
        deg_bank = deg_psum.tile([P, DEG_COLUMNS[0] + DEG_COLUMNS[1]], F32)
        deg_parts = [deg_bank[:, : DEG_COLUMNS[0]], deg_bank[:, DEG_COLUMNS[0] :]]

        x_rows = {}
        x_cols = {}
        raw = {}
        grouped = {}
        deg = {}
        root = {}
        dinv_spread = {}
        dinv = {}
        dinv_msg = {}
        picked = {}
        grouped_msg = {}
        xw = {}
        acc = {}

        def load_rows(g, a, first, count):
            chunk = raw_pool.tile([P, PACK, count * UNIT], BF16, name="raw%d" % count, bufs=RAW_BUFS[count])
            rows = flows[g, a * P * PACK : (a + 1) * P * PACK, :].rearrange("(p t) c -> p t c", t=PACK)
            if count == UNITS:
                for t in range(0, PACK, 2):
                    nc.sync.dma_start(out=chunk[:, t : t + 2, :], in_=rows[:, t : t + 2, :])
            else:
                nc.sync.dma_start(out=chunk[:], in_=rows[:, :, first * UNIT : (first + count) * UNIT])
            for i in range(count):
                raw[g, a, first + i] = chunk[:, :, i * UNIT : (i + 1) * UNIT]

        def load_features(g):
            x_rows[g] = keep.tile([P, NODE_TILES, FEATURES], BF16, name="x_rows%d" % g)
            nc.sync.dma_start(
                out=x_rows[g][:].rearrange("p (a t) k -> p a t k", t=PACK),
                in_=x_gcn1[g].rearrange("(a p t) k -> p a t k", p=P, t=PACK),
            )

        def transpose_features(g, a):
            if a == 0:
                x_cols[g] = keep.tile([P, NODE_TILES, P], BF16, name="x_cols%d" % g)
            turned = work_psum.tile([P, PACK, P], BF16, tag="work")
            for t in range(PACK):
                nc.tensor.transpose(turned[:, t, :], x_rows[g][:, a * PACK + t, :], identity[:])
            nc.scalar.copy(out=x_cols[g][:, a * PACK : (a + 1) * PACK, :], in_=turned[:])

        def degree_sums(g, a, u, part, rows):
            for n in range(u * UNIT_TILES, (u + 1) * UNIT_TILES):
                first = part * NODE_TILES + n
                for t in rows:
                    nc.tensor.matmul(
                        out=deg_parts[g][:, first : first + COPIES[g]],
                        lhsT=raw[g, a, u][:, t, (n % UNIT_TILES) * P : (n % UNIT_TILES + 1) * P],
                        rhs=ones[:, 0 : COPIES[g]],
                        start=(t == rows[0]),
                        stop=(t == rows[-1]),
                    )

        def degree_unit(g, a, u):
            degree_sums(g, a, u, a, range(PACK))

        def degree_half(g, a, u, half):
            degree_sums(g, a, u, 2 * a - 1 + half, (2 * half, 2 * half + 1))

        def regroup(copy, g, a, u, first, last):
            copy(
                out=grouped[g, a, u][:, first:last, :].rearrange("p (c i) t -> p c t i", i=RUN),
                in_=raw[g, a, u][:, :, first:last].rearrange("p t (c i) -> p c t i", i=RUN),
            )

        def open_unit(g, a, u):
            if (g, a, u) not in grouped:
                grouped[g, a, u] = grouped_pool.tile([P, UNIT, PACK], BF16, name="grouped", align_bytes=64)

        def regroup_unit(g, a, u, vector_columns):
            open_unit(g, a, u)
            regroup(nc.scalar.copy, g, a, u, vector_columns, UNIT)

        def regroup_vector(g, a, u, vector_columns):
            if vector_columns > 0:
                open_unit(g, a, u)
                regroup(nc.vector.tensor_copy, g, a, u, 0, vector_columns)

        def quantise_unit(g, a, u):
            cols = slice(u * UNIT, (u + 1) * UNIT)
            nc.vector.quantize_mx(
                out=flow_codes[g][:, a, cols].bitcast(FP8X4),
                scales=flow_scales[g][:, a, cols],
                in_=grouped[g, a, u][:].rearrange("p c t -> p (c t)"),
            )

        def degrees(g):
            deg[g] = small.tile([P, NODE_TILES], F32, name="deg")
            nc.vector.tensor_reduce(
                out=deg[g][:],
                in_=deg_parts[g][:, : DEG_PARTS[g] * NODE_TILES].rearrange("p (k n) -> p n k", n=NODE_TILES),
                axis=AXIS.X,
                op=ALU.add,
            )

        def roots(g):
            safe = small.tile([P, NODE_TILES], F32, name="safe")
            nc.vector.scalar_tensor_tensor(
                out=safe[:], in0=deg[g][:], scalar=0.0, in1=deg[g][:], op0=ALU.is_le, op1=ALU.add
            )
            root[g] = small.tile([P, NODE_TILES], F32, name="root")
            nc.scalar.sqrt(root[g][:], safe[:])

        def inverses(g):
            inverse = small.tile([P, NODE_TILES], F32, name="inverse")
            nc.vector.reciprocal(inverse[:], root[g][:])
            dinv[g] = small.tile([P, NODE_TILES], F32, name="dinv")
            nc.vector.scalar_tensor_tensor(
                out=dinv[g][:], in0=deg[g][:], scalar=0.0, in1=inverse[:], op0=ALU.is_gt, op1=ALU.mult
            )
            dinv_spread[g] = small.tile([P, NODE_TILES, PACK], F32, name="dinv_spread")
            nc.vector.tensor_tensor(
                out=dinv_spread[g][:],
                in0=dinv[g][:].unsqueeze(2).to_broadcast([P, NODE_TILES, PACK]),
                in1=residue[:].unsqueeze(1).to_broadcast([P, NODE_TILES, PACK]),
                op=ALU.mult,
            )

        def pick_inverses(g):
            picked[g] = work_psum.tile([P, NODE_TILES, PACK], F32, name="picked", tag="work")
            nc.tensor.matmul(
                out=picked[g][:].rearrange("p n t -> p (n t)"),
                lhsT=fours[:].rearrange("p q j -> p (q j)"),
                rhs=dinv_spread[g][:].rearrange("p n t -> p (n t)"),
                start=True,
                stop=True,
            )

        def message_inverses(g):
            dinv_msg[g] = small.tile([P, NODE_TILES], F32, name="dinv_msg")
            for q in range(QUADS):
                part = slice(QUAD * q, QUAD * (q + 1))
                nc.vector.tensor_copy(
                    out=dinv_msg[g][part, :].rearrange("p (a t) -> p a t", t=PACK),
                    in_=picked[g][part, q : NODE_TILES : QUADS, :],
                )

        def features_times_weights(g, a):
            for h in range(CHANNELS // HALF):
                xw[g, a, h] = work_psum.tile([P, PACK, HALF], F32, name="xw", tag="work")
                for t in range(PACK):
                    nc.tensor.matmul(
                        out=xw[g, a, h][:, t, :],
                        lhsT=x_cols[g][:, a * PACK + t, :],
                        rhs=w2_sb[:, h * HALF : (h + 1) * HALF],
                        start=True,
                        stop=True,
                    )

        def scale_messages(g, a):
            if a == 0:
                grouped_msg[g] = keep.tile([P, PASSES, CHANNELS, PACK], BF16, name="grouped_msg", align_bytes=64)
            for h in range(CHANNELS // HALF):
                nc.vector.tensor_tensor(
                    out=grouped_msg[g][:, a, h * HALF : (h + 1) * HALF, :],
                    in0=xw[g, a, h][:].rearrange("p t i -> p i t"),
                    in1=dinv_msg[g][:, a * PACK : (a + 1) * PACK].unsqueeze(1).to_broadcast([P, HALF, PACK]),
                    op=ALU.mult,
                )

        def quantise_messages(g, a):
            nc.vector.quantize_mx(
                out=msg_codes[g][:, a, :].bitcast(FP8X4),
                scales=msg_scales[g][:, a, :],
                in_=grouped_msg[g][:, a, :, :].rearrange("p i t -> p (i t)"),
            )

        def product_passes(g, n, passes):
            rows = slice(n * P, (n + 1) * P)
            for a in passes:
                nc.tensor.matmul_mx(
                    out=acc[g, n],
                    lhsT=flow_codes[g][:, a, rows].bitcast(FP8X4),
                    lhsT_scale=flow_scales[g][:, a, rows],
                    rhs=msg_codes[g][:, a, :].bitcast(FP8X4),
                    rhs_scale=msg_scales[g][:, a, :],
                    start=(a == 0),
                    stop=(a == PASSES - 1),
                )

        def multiply(g, j):
            if g == 1 and j < 4:
                bank = work_psum.tile([P, PAIR, CHANNELS], F32, name="bank", tag="work")
            else:
                bank = acc_psum.tile([P, PAIR, CHANNELS], F32, name="bank")
            for i in range(PAIR):
                acc[g, PAIR * j + i] = bank[:, i, :]
                product_passes(g, PAIR * j + i, range(PASSES))

        def begin_last(n):
            bank = work_psum.tile([P, CHANNELS], F32, name="last", tag="work")
            acc[1, n] = bank[:]
            product_passes(1, n, range(PASSES - 1))

        def end_last(n):
            product_passes(1, n, [PASSES - 1])

        def finish(g, j):
            result = result_pool.tile([P, PAIR, CHANNELS], F32, name="result")
            for i in range(PAIR):
                n = j * PAIR + i
                nc.vector.scalar_tensor_tensor(
                    out=result[:, i, :],
                    in0=acc[g, n],
                    scalar=dinv[g][:, n : n + 1],
                    in1=bias[:],
                    op0=ALU.mult,
                    op1=ALU.add,
                )
            nc.sync.dma_start(
                out=out[g, j * PAIR * P : (j + 1) * PAIR * P, :].rearrange("(i p) c -> p i c", p=P),
                in_=result[:],
            )

        def normalise(g):
            degrees(g)
            roots(g)
            inverses(g)
            pick_inverses(g)
            message_inverses(g)

        def messages(g, beside):
            for a in range(PASSES):
                features_times_weights(g, a)
                beside(a)
                scale_messages(g, a)
            for a in range(PASSES):
                quantise_messages(g, a)

        load_rows(0, 0, 0, 1)
        load_rows(0, 0, 1, 1)
        halves = [(g, a, first) for g in range(GRAPHS) for a in range(PASSES) for first in (0, UNITS // 2)]
        halves = halves[1 : 2 * PASSES + 2]
        for g, a, first in halves[:3]:
            load_rows(g, a, first, 2)
        ones = const.tile([P, P], BF16)
        nc.vector.memset(ones[:], 1.0)
        scratch = const.tile([P, 1], F32)
        nc.vector.memset(scratch[:], 1.0)
        nc.scalar.sqrt(scratch[:], scratch[:])
        nc.vector.memset(bias_row[:], 0.0)
        identity_f32 = const.tile([P, P], F32)
        make_identity(nc, identity_f32[:])
        identity = const.tile([P, P], BF16)
        nc.vector.tensor_copy(out=identity[:], in_=identity_f32[:])
        four = const.tile([P, QUAD], F32)
        nc.vector.tensor_reduce(
            out=four[:], in_=identity_f32[:].rearrange("p (j t) -> p j t", t=PACK), axis=AXIS.X, op=ALU.add
        )
        fours = const.tile([P, QUADS, QUAD], F32)
        nc.vector.tensor_copy(out=fours[:], in_=four[:].unsqueeze(1).to_broadcast([P, QUADS, QUAD]))
        residue = const.tile([P, PACK], F32)
        nc.vector.tensor_reduce(
            out=residue[:], in_=identity_f32[:].rearrange("p (j t) -> p t j", t=PACK), axis=AXIS.X, op=ALU.add
        )
        nc.sync.dma_start(out=w2_sb[:], in_=W2)
        nc.sync.dma_start(out=bias_row[0:1, :], in_=b2.unsqueeze(0))
        load_rows(*halves[3], 2)
        halves = halves[4:]

        flows_of_0 = [(0, a, u) for a in range(PASSES) for u in range(UNITS)]
        for k, unit in enumerate(flows_of_0):
            degree_unit(*unit)
            regroup_unit(*unit, 256)
            regroup_vector(*unit, 256)
            if k > 0:
                quantise_unit(*flows_of_0[k - 1])
            if k >= 3 and k % 2 == 1 and halves:
                load_rows(*halves.pop(0), 2)
                if len(halves) == 2:
                    load_features(0)
            if k == 6:
                spread = work_psum.tile([P, CHANNELS], F32, tag="work")
                nc.tensor.matmul(out=spread[:], lhsT=ones[:], rhs=bias_row[:], start=True, stop=True)
                nc.vector.tensor_copy(out=bias[:], in_=spread[:])
        for a in range(1, PASSES):
            load_rows(1, a, 0, UNITS)
        load_features(1)

        ctx.enter_context(tc.manual_schedule(engines={mybir.EngineType.PE}))

        for a in range(PASSES):
            transpose_features(0, a)
        normalise(0)
        messages(0, lambda a: degree_unit(1, 0, a))
        quantise_unit(*flows_of_0[-1])

        flows_of_1 = [(1, a, u) for a in range(2) for u in range(UNITS)]
        flows_of_1 += [(1, a, u) for u in range(UNITS) for a in range(2, PASSES)]

        def step(k):
            share = 160 if k < 2 else 128 if k < 6 else 96 if k < 8 else 0
            regroup_unit(*flows_of_1[k], share)
            regroup_vector(*flows_of_1[k], share)
            if k > 0:
                quantise_unit(*flows_of_1[k - 1])

        for k in range(6):
            step(k)
            for u in range(UNITS):
                degree_half(1, 1 + k // 2, u, k % 2)
            if k % 2 == 0:
                multiply(0, k // 2)
            else:
                finish(0, k // 2)

        def next_product(a):
            multiply(0, 3 + a)
            if a > 0:
                finish(0, 2 + a)

        for a in range(PASSES):
            transpose_features(1, a)
        with tc.high_priority():
            normalise(1)
        messages(1, next_product)
        for k in range(6, 16):
            step(k)
            if k == 6:
                multiply(0, 7)
                finish(0, 6)
            if k == 7:
                finish(0, 7)
            if k >= 10 and k % 2 == 0:
                multiply(1, k - 10)
                multiply(1, k - 9)
            if k >= 11 and k % 2 == 1:
                finish(1, k - 11)
                finish(1, k - 10)
        for n in range(12, 16):
            begin_last(n)
        quantise_unit(*flows_of_1[-1])
        for n in range(12, 16):
            end_last(n)
        finish(1, 6)
        finish(1, 7)
